import numpy as np
import ml_dtypes


def mxq(x, axis, fmt="e4m3"):
    dtype, down = {"e4m3": (ml_dtypes.float8_e4m3fn, 7), "e5m2": (ml_dtypes.float8_e5m2, 14)}[fmt]
    v = np.moveaxis(np.asarray(x, np.float32).astype(ml_dtypes.bfloat16).astype(np.float64), axis, -1)
    blocks = v.reshape(v.shape[:-1] + (-1, 32))
    amax = np.abs(blocks).max(-1, keepdims=True)
    byte = np.maximum(np.where(amax > 0, np.frexp(amax)[1] - 1 + 127, 0) - down, 1)
    scale = np.exp2(byte - 127.0)
    codes = (blocks / scale).astype(np.float32).astype(dtype).astype(np.float64)
    return np.moveaxis((codes * scale).reshape(v.shape), -1, axis)


WIDE = False


def mx_kscale(k):
    if not WIDE:
        return np.ones(k)
    levels = np.array([10, -10, 5, -5, 0])
    a = np.random.permutation(np.resize(levels, k // 512 * 4)).reshape(k // 512, 4)
    idx = np.arange(k)
    return np.exp2(a[idx // 512, idx % 128 // 32])


BF16 = ml_dtypes.bfloat16


def bf(x):
    return np.asarray(x, np.float32).astype(BF16)


def f64(x):
    return np.asarray(x).astype(np.float64)


B, H, SQ, SK, DK = 1, 4, 4096, 1024, 128
D = H * DK


def setup_inputs():
    s = mx_kscale(D)
    g = np.random.standard_normal
    return {"q": bf(g((B, H, SQ, DK)) * 1.4),
            "k": bf(g((B, H, SK, DK)) * 1.4),
            "image_feat": bf(g((B, SK, D)) * 0.13 * np.sqrt(SK) * s),
            "W3": bf(g((D, D)) * 2.0 / np.sqrt(D) / s[None, :]),
            "b3": bf(g(D) * 0.4)}


def reference(q, k, image_feat, W3, b3):
    imf = (mxq(f64(image_feat), 2, "e4m3") @ mxq(f64(W3), 1, "e4m3").T) + f64(b3)
    imf = imf.reshape(B, SK, H, DK).transpose(0, 2, 1, 3)
    s = f64(q) @ f64(k).transpose(0, 1, 3, 2) / np.sqrt(DK)
    e = np.exp(s - s.max(-1, keepdims=True))
    return (mxq(e, 3, "e4m3") @ mxq(imf, 2, "e4m3")) / e.sum(-1, keepdims=True)

@@ -1,0 +1,289 @@
+from contextlib import ExitStack
+import math
+
+import concourse.mybir as mybir
+from concourse.masks import make_identity
+
+F32 = mybir.dt.float32
+BF16 = mybir.dt.bfloat16
+U32 = mybir.dt.uint32
+U8 = mybir.dt.uint8
+FP8X4 = mybir.dt.float8_e4m3fn_x4
+ALU = mybir.AluOpType
+ACTF = mybir.ActivationFunctionType
+AX = mybir.AxisListType
+
+P = 128
+H, SQ, SK, DK = 4, 4096, 1024, 128
+D = H * DK
+NQ = SQ // P
+NT = H * NQ
+NB = SK // P
+GRP = 4
+SCALE = 1.0 / math.sqrt(DK)
+FLOPS = 2 * SK * D * D + 2 * 2 * H * SQ * SK * DK
+PIN = False
+DVE_COPY_EVERY = 4
+
+
+def tile_multiheadedattention_pa_t_kernel(tc, q, k, image_feat, W3, b3, out):
+    nc = tc.nc
+    qf = q.flatten_outer_dims()
+    kf = k.flatten_outer_dims()
+    xf = image_feat.flatten_outer_dims()
+    of = out.flatten_outer_dims()
+
+    with ExitStack() as ctx:
+        const = ctx.enter_context(tc.tile_pool(name="const", bufs=1))
+        qraw_pool = ctx.enter_context(tc.tile_pool(name="qraw", bufs=H))
+        qt_pool = ctx.enter_context(tc.tile_pool(name="qt", bufs=2))
+        work = ctx.enter_context(tc.tile_pool(name="work", bufs=3))
+        stat = ctx.enter_context(tc.tile_pool(name="stat", bufs=4))
+        ps_s = ctx.enter_context(tc.psum_pool(name="ps_s", bufs=4))
+        ps_t = ctx.enter_context(tc.psum_pool(name="ps_t", bufs=2))
+        ps_o = ctx.enter_context(tc.psum_pool(name="ps_o", bufs=1))
+        ps_p = ctx.enter_context(tc.psum_pool(name="ps_p", bufs=1))
+
+        ident_b = const.tile([P, P], BF16, name="ident_b")
+        make_identity(nc, ident_b[:])
+        ident_f = const.tile([P, P], F32, name="ident_f")
+        make_identity(nc, ident_f[:])
+
+        x_raw = const.tile([P, NB * D], BF16, name="x_raw")
+        w_raw = const.tile([P, H * D], BF16, name="w_raw")
+        b3bc = const.tile([P, D], BF16, name="b3bc")
+        k_raw = const.tile([P, H, NB, DK], BF16, name="k_raw")
+        q_raws = []
+        for h in range(H):
+            if h == 1:
+                nc.sync.dma_start(out=x_raw[:], in_=xf.rearrange("(p n) c -> p (n c)", n=NB))
+                nc.sync.dma_start(
+                    out=w_raw[:].rearrange("p (n c) -> p n c", n=H),
+                    in_=W3.rearrange("(n p) c -> p n c", p=P),
+                )
+                nc.sync.dma_start(out=b3bc[:], in_=b3.partition_broadcast(P))
+            nc.sync.dma_start(
+                out=k_raw[:, h, :, :],
+                in_=kf[h * SK : (h + 1) * SK, :].rearrange("(p n) d -> p n d", n=NB),
+            )
+            q_raw = qraw_pool.tile([P, NQ, DK], BF16, name="q_raw", tag="q_raw")
+            nc.sync.dma_start(
+                out=q_raw[:],
+                in_=qf[h * SQ : (h + 1) * SQ, :].rearrange("(p n) d -> p n d", n=NQ),
+            )
+            q_raws.append(q_raw)
+
+        kT = const.tile([P, H, SK], BF16, name="kT")
+        qTs = {}
+
+        def prep_k(h):
+            pk = ps_p.tile([P, NB, P], BF16, name="pk", tag="prep")
+            for n in range(NB):
+                nc.tensor.transpose(pk[:, n, :], k_raw[:, h, n, :], ident_b[:])
+            nc.vector.tensor_copy(
+                out=kT[:, h, :].rearrange("p (n r) -> p n r", n=NB), in_=pk[:]
+            )
+
+        def prep_q(h, r):
+            if r == 0:
+                qTs[h] = qt_pool.tile([P, NQ, P], BF16, name="qT", tag="qT")
+            pq = ps_p.tile([P, 8, P], BF16, name="pq", tag="prep")
+            for a in range(8):
+                nc.tensor.transpose(pq[:, a, :], q_raws[h][:, 8 * r + a, :], ident_b[:])
+            nc.vector.tensor_copy(out=qTs[h][:, 8 * r : 8 * r + 8, :], in_=pq[:])
+
+        prep_k(0)
+        for r in range(4):
+            prep_q(0, r)
+
+        def words_to_k_on_partitions(raw, n_tiles, grouped):
+            raw32 = raw[:].bitcast(F32)
+            grouped32 = grouped[:].bitcast(F32)
+            for pair in range(n_tiles // 2):
+                px = ps_s.tile([P, 2, 2, P], F32, name="px", tag="s")
+                for a in range(2):
+                    for u in range(2):
+                        c0 = (2 * pair + a) * (D // 2) + u * P
+                        nc.tensor.transpose(px[:, a, u, :], raw32[:, c0 : c0 + P], ident_f[:])
+                nc.vector.tensor_copy(
+                    out=grouped32[:, pair * 512 : (pair + 1) * 512].rearrange(
+                        "p (a r u) -> p a r u", a=2, u=2
+                    ),
+                    in_=px[:].rearrange("p a u r -> p a r u"),
+                )
+
+        xg = const.tile([P, SK * 4], BF16, name="xg", align_bytes=64)
+        wg = const.tile([P, D * 4], BF16, name="wg", align_bytes=64)
+        xc = const.tile([P, SK], U32, name="xc", align_bytes=64)
+        xs = const.tile([P, SK], U8, name="xs", align_bytes=64)
+        wc = const.tile([P, D], U32, name="wc", align_bytes=64)
+        ws = const.tile([P, D], U8, name="ws", align_bytes=64)
+        words_to_k_on_partitions(x_raw, NB, xg)
+        words_to_k_on_partitions(w_raw, H, wg)
+        nc.vector.quantize_mx(out=xc[:].bitcast(FP8X4), scales=xs[:], in_=xg[:])
+        nc.vector.quantize_mx(out=wc[:].bitcast(FP8X4), scales=ws[:], in_=wg[:])
+
+        ig = const.tile([P, 2, D, 4], BF16, name="ig", align_bytes=64)
+        ic = const.tile([P, 2, D], U32, name="ic", align_bytes=64)
+        isc = const.tile([P, 2, D], U8, name="isc", align_bytes=64)
+        for g in range(2):
+            for h in range(H):
+                hs = slice(h * DK, (h + 1) * DK)
+                pi = ps_s.tile([P, 4, DK], F32, name="pi", tag="s")
+                for t in range(4):
+                    bs = slice((4 * g + t) * P, (4 * g + t + 1) * P)
+                    nc.tensor.matmul_mx(
+                        out=pi[:, t, :],
+                        lhsT=xc[:, bs].bitcast(FP8X4),
+                        lhsT_scale=xs[:, bs],
+                        rhs=wc[:, hs].bitcast(FP8X4),
+                        rhs_scale=ws[:, hs],
+                        start=True,
+                        stop=True,
+                    )
+                nc.vector.tensor_tensor(
+                    out=ig[:, g, hs, :],
+                    in0=pi[:].rearrange("p t o -> p o t"),
+                    in1=b3bc[:, hs].unsqueeze(2).to_broadcast([P, DK, 4]),
+                    op=ALU.add,
+                )
+            nc.vector.quantize_mx(
+                out=ic[:, g, :].bitcast(FP8X4),
+                scales=isc[:, g, :],
+                in_=ig[:, g, :, :].rearrange("p o t -> p (o t)"),
+            )
+
+        s_t, nb_t, e_t, et_t, eg_t, ec_t, es_t, rs_t, pv_t = {}, {}, {}, {}, {}, {}, {}, {}, {}
+
+        def scores(i):
+            h, n = divmod(i, NQ)
+            banks = []
+            for c in range(2):
+                s = ps_s.tile([P, 512], F32, name="s", tag="s")
+                nc.tensor.matmul(
+                    out=s[:],
+                    lhsT=qTs[h][:, n, :],
+                    rhs=kT[:, h, c * 512 : (c + 1) * 512],
+                    start=True,
+                    stop=True,
+                )
+                banks.append(s)
+            s_t[i] = banks
+
+        def row_max(i):
+            mx = stat.tile([P, 2], F32, name="mx", tag="mx")
+            for c in range(2):
+                nc.vector.tensor_reduce(out=mx[:, c : c + 1], in_=s_t[i][c][:], axis=AX.X, op=ALU.max)
+            nb = stat.tile([P, 1], F32, name="nb", tag="nb")
+            nc.vector.tensor_scalar(
+                out=nb[:], in0=mx[:, 0:1], scalar1=mx[:, 1:2], scalar2=-SCALE, op0=ALU.max, op1=ALU.mult
+            )
+            nb_t[i] = nb
+
+        def exponent(i):
+            if i % GRP == 0:
+                rs_t[i // GRP] = stat.tile([P, GRP, 2], F32, name="rs", tag="rs")
+            rs = rs_t[i // GRP]
+            e = work.tile([P, SK], BF16, name="e", tag="e")
+            for c in range(2):
+                nc.scalar.activation(
+                    out=e[:, c * 512 : (c + 1) * 512],
+                    in_=s_t[i][c][:],
+                    func=ACTF.Exp,
+                    bias=nb_t[i][:],
+                    scale=SCALE,
+                    accum_out=rs[:, i % GRP, c : c + 1],
+                )
+            e_t[i] = e
+
+        def flip(i):
+            et = ps_t.tile([P, NB, P], BF16, name="et", tag="et")
+            for b in range(NB):
+                nc.tensor.transpose(et[:, b, :], e_t[i][:, b * P : (b + 1) * P], ident_b[:])
+            et_t[i] = et
+
+        def regroup(i):
+            eg = work.tile([P, 2, P, 4], BF16, name="eg", tag="eg", align_bytes=64)
+            src = et_t[i][:].rearrange("p (g t) r -> p g r t", g=2)
+            if i % DVE_COPY_EVERY == DVE_COPY_EVERY - 1:
+                nc.vector.tensor_copy(out=eg[:], in_=src)
+            else:
+                nc.scalar.copy(out=eg[:], in_=src)
+            eg_t[i] = eg
+
+        def quantise(i):
+            ec = work.tile([P, 2 * P], U32, name="ec", tag="ec", align_bytes=64)
+            es = work.tile([P, 2 * P], U8, name="es", tag="es", align_bytes=64)
+            nc.vector.quantize_mx(
+                out=ec[:].bitcast(FP8X4),
+                scales=es[:],
+                in_=eg_t[i][:].rearrange("p g r t -> p (g r t)"),
+            )
+            ec_t[i] = ec
+            es_t[i] = es
+
+        def pool_features(i):
+            h = i // NQ
+            if i % GRP == 0:
+                pv_t[i // GRP] = ps_o.tile([P, GRP, DK], F32, name="pv", tag="pv")
+            pv = pv_t[i // GRP]
+            hs = slice(h * DK, (h + 1) * DK)
+            for g in range(2):
+                gs = slice(g * P, (g + 1) * P)
+                nc.tensor.matmul_mx(
+                    out=pv[:, i % GRP, :],
+                    lhsT=ec_t[i][:, gs].bitcast(FP8X4),
+                    lhsT_scale=es_t[i][:, gs],
+                    rhs=ic[:, g, hs].bitcast(FP8X4),
+                    rhs_scale=isc[:, g, hs],
+                    start=(g == 0),
+                    stop=(g == 1),
+                )
+
+        def finish(grp):
+            h, m = divmod(grp, NQ // GRP)
+            rsum = stat.tile([P, GRP], F32, name="rsum", tag="rsum")
+            nc.vector.tensor_reduce(out=rsum[:], in_=rs_t[grp][:], axis=AX.X, op=ALU.add)
+            rcp = stat.tile([P, GRP], F32, name="rcp", tag="rcp")
+            nc.vector.reciprocal(out=rcp[:], in_=rsum[:])
+            o_sb = work.tile([P, GRP, DK], F32, name="o_sb", tag="o_sb")
+            nc.vector.tensor_tensor(
+                out=o_sb[:],
+                in0=pv_t[grp][:],
+                in1=rcp[:].unsqueeze(2).to_broadcast([P, GRP, DK]),
+                op=ALU.mult,
+            )
+            nc.sync.dma_start(
+                out=of[h * SQ : (h + 1) * SQ, :].rearrange("(p n) d -> p n d", n=NQ)[
+                    :, m * GRP : (m + 1) * GRP, :
+                ],
+                in_=o_sb[:],
+            )
+
+        def live(i):
+            return 0 <= i < NT
+
+        if PIN:
+            ctx.enter_context(tc.manual_schedule())
+        for step in range(-1, NT + 2):
+            if live(step - 2):
+                quantise(step - 2)
+            if live(step + 1):
+                scores(step + 1)
+                row_max(step + 1)
+            if live(step):
+                exponent(step)
+            if live(step - 1):
+                flip(step - 1)
+                regroup(step - 1)
+            if live(step - 2):
+                pool_features(step - 2)
+                if (step - 2) % GRP == GRP - 1:
+                    finish((step - 2) // GRP)
+            if live(step):
+                h, n = divmod(step, NQ)
+                if h + 1 < H:
+                    if n == 8:
+                        prep_k(h + 1)
+                    if n in (12, 16, 20, 24):
+                        prep_q(h + 1, (n - 12) // 4)

@@ -22,8 +22,8 @@ NB = SK // P
 GRP = 4
 SCALE = 1.0 / math.sqrt(DK)
 FLOPS = 2 * SK * D * D + 2 * 2 * H * SQ * SK * DK
-PIN = False
-DVE_COPY_EVERY = 4
+QLAG = 3
+EC_BUFS = 20
 
 
 def tile_multiheadedattention_pa_t_kernel(tc, q, k, image_feat, W3, b3, out):
@@ -37,8 +37,10 @@ def tile_multiheadedattention_pa_t_kernel(tc, q, k, image_feat, W3, b3, out):
         const = ctx.enter_context(tc.tile_pool(name="const", bufs=1))
         qraw_pool = ctx.enter_context(tc.tile_pool(name="qraw", bufs=H))
         qt_pool = ctx.enter_context(tc.tile_pool(name="qt", bufs=2))
-        work = ctx.enter_context(tc.tile_pool(name="work", bufs=3))
+        work = ctx.enter_context(tc.tile_pool(name="work", bufs=4))
+        codes = ctx.enter_context(tc.tile_pool(name="codes", bufs=EC_BUFS))
         stat = ctx.enter_context(tc.tile_pool(name="stat", bufs=4))
+        sums = ctx.enter_context(tc.tile_pool(name="sums", bufs=8))
         ps_s = ctx.enter_context(tc.psum_pool(name="ps_s", bufs=4))
         ps_t = ctx.enter_context(tc.psum_pool(name="ps_t", bufs=2))
         ps_o = ctx.enter_context(tc.psum_pool(name="ps_o", bufs=1))
@@ -55,22 +57,24 @@ def tile_multiheadedattention_pa_t_kernel(tc, q, k, image_feat, W3, b3, out):
         k_raw = const.tile([P, H, NB, DK], BF16, name="k_raw")
         q_raws = []
         for h in range(H):
-            if h == 1:
+            nc.sync.dma_start(
+                out=k_raw[:, h, :, :],
+                in_=kf[h * SK : (h + 1) * SK, :].rearrange("(p n) d -> p n d", n=NB),
+            )
+            q_raw = qraw_pool.tile([P, NQ, DK], BF16, name="q_raw", tag="q_raw")
+            q_src = qf[h * SQ : (h + 1) * SQ, :].rearrange("(p n) d -> p n d", n=NQ)
+            if h == 0:
+                for r in range(2):
+                    nc.sync.dma_start(out=q_raw[:, 8 * r : 8 * r + 8, :], in_=q_src[:, 8 * r : 8 * r + 8, :])
                 nc.sync.dma_start(out=x_raw[:], in_=xf.rearrange("(p n) c -> p (n c)", n=NB))
                 nc.sync.dma_start(
                     out=w_raw[:].rearrange("p (n c) -> p n c", n=H),
                     in_=W3.rearrange("(n p) c -> p n c", p=P),
                 )
                 nc.sync.dma_start(out=b3bc[:], in_=b3.partition_broadcast(P))
-            nc.sync.dma_start(
-                out=k_raw[:, h, :, :],
-                in_=kf[h * SK : (h + 1) * SK, :].rearrange("(p n) d -> p n d", n=NB),
-            )
-            q_raw = qraw_pool.tile([P, NQ, DK], BF16, name="q_raw", tag="q_raw")
-            nc.sync.dma_start(
-                out=q_raw[:],
-                in_=qf[h * SQ : (h + 1) * SQ, :].rearrange("(p n) d -> p n d", n=NQ),
-            )
+                nc.sync.dma_start(out=q_raw[:, 16:32, :], in_=q_src[:, 16:32, :])
+            else:
+                nc.sync.dma_start(out=q_raw[:], in_=q_src)
             q_raws.append(q_raw)
 
         kT = const.tile([P, H, SK], BF16, name="kT")
@@ -92,66 +96,88 @@ def tile_multiheadedattention_pa_t_kernel(tc, q, k, image_feat, W3, b3, out):
                 nc.tensor.transpose(pq[:, a, :], q_raws[h][:, 8 * r + a, :], ident_b[:])
             nc.vector.tensor_copy(out=qTs[h][:, 8 * r : 8 * r + 8, :], in_=pq[:])
 
-        prep_k(0)
-        for r in range(4):
-            prep_q(0, r)
-
-        def words_to_k_on_partitions(raw, n_tiles, grouped):
-            raw32 = raw[:].bitcast(F32)
-            grouped32 = grouped[:].bitcast(F32)
-            for pair in range(n_tiles // 2):
-                px = ps_s.tile([P, 2, 2, P], F32, name="px", tag="s")
-                for a in range(2):
-                    for u in range(2):
-                        c0 = (2 * pair + a) * (D // 2) + u * P
-                        nc.tensor.transpose(px[:, a, u, :], raw32[:, c0 : c0 + P], ident_f[:])
-                nc.vector.tensor_copy(
-                    out=grouped32[:, pair * 512 : (pair + 1) * 512].rearrange(
-                        "p (a r u) -> p a r u", a=2, u=2
-                    ),
-                    in_=px[:].rearrange("p a u r -> p a r u"),
-                )
-
         xg = const.tile([P, SK * 4], BF16, name="xg", align_bytes=64)
         wg = const.tile([P, D * 4], BF16, name="wg", align_bytes=64)
         xc = const.tile([P, SK], U32, name="xc", align_bytes=64)
         xs = const.tile([P, SK], U8, name="xs", align_bytes=64)
         wc = const.tile([P, D], U32, name="wc", align_bytes=64)
         ws = const.tile([P, D], U8, name="ws", align_bytes=64)
-        words_to_k_on_partitions(x_raw, NB, xg)
-        words_to_k_on_partitions(w_raw, H, wg)
-        nc.vector.quantize_mx(out=xc[:].bitcast(FP8X4), scales=xs[:], in_=xg[:])
-        nc.vector.quantize_mx(out=wc[:].bitcast(FP8X4), scales=ws[:], in_=wg[:])
-
         ig = const.tile([P, 2, D, 4], BF16, name="ig", align_bytes=64)
         ic = const.tile([P, 2, D], U32, name="ic", align_bytes=64)
         isc = const.tile([P, 2, D], U8, name="isc", align_bytes=64)
-        for g in range(2):
-            for h in range(H):
-                hs = slice(h * DK, (h + 1) * DK)
-                pi = ps_s.tile([P, 4, DK], F32, name="pi", tag="s")
-                for t in range(4):
-                    bs = slice((4 * g + t) * P, (4 * g + t + 1) * P)
-                    nc.tensor.matmul_mx(
-                        out=pi[:, t, :],
-                        lhsT=xc[:, bs].bitcast(FP8X4),
-                        lhsT_scale=xs[:, bs],
-                        rhs=wc[:, hs].bitcast(FP8X4),
-                        rhs_scale=ws[:, hs],
-                        start=True,
-                        stop=True,
-                    )
-                nc.vector.tensor_tensor(
-                    out=ig[:, g, hs, :],
-                    in0=pi[:].rearrange("p t o -> p o t"),
-                    in1=b3bc[:, hs].unsqueeze(2).to_broadcast([P, DK, 4]),
-                    op=ALU.add,
+
+        def words_to_k_on_partitions(raw, grouped, pair):
+            raw32 = raw[:].bitcast(F32)
+            grouped32 = grouped[:].bitcast(F32)
+            px = ps_p.tile([P, 2, 2, P], F32, name="px", tag="prep")
+            for a in range(2):
+                for u in range(2):
+                    c0 = (2 * pair + a) * (D // 2) + u * P
+                    nc.tensor.transpose(px[:, a, u, :], raw32[:, c0 : c0 + P], ident_f[:])
+            nc.vector.tensor_copy(
+                out=grouped32[:, pair * 512 : (pair + 1) * 512].rearrange(
+                    "p (a r u) -> p a r u", a=2, u=2
+                ),
+                in_=px[:].rearrange("p a u r -> p a r u"),
+            )
+
+        def quantise_x(half):
+            nc.vector.quantize_mx(
+                out=xc[:, half * 512 : (half + 1) * 512].bitcast(FP8X4),
+                scales=xs[:, half * 512 : (half + 1) * 512],
+                in_=xg[:, half * 2048 : (half + 1) * 2048],
+            )
+
+        def quantise_w():
+            nc.vector.quantize_mx(out=wc[:].bitcast(FP8X4), scales=ws[:], in_=wg[:])
+
+        def project(g, h):
+            hs = slice(h * DK, (h + 1) * DK)
+            pi = ps_p.tile([P, 4, DK], F32, name="pi", tag="prep")
+            for t in range(4):
+                bs = slice((4 * g + t) * P, (4 * g + t + 1) * P)
+                nc.tensor.matmul_mx(
+                    out=pi[:, t, :],
+                    lhsT=xc[:, bs].bitcast(FP8X4),
+                    lhsT_scale=xs[:, bs],
+                    rhs=wc[:, hs].bitcast(FP8X4),
+                    rhs_scale=ws[:, hs],
+                    start=True,
+                    stop=True,
                 )
+            nc.vector.tensor_tensor(
+                out=ig[:, g, hs, :],
+                in0=pi[:].rearrange("p t o -> p o t"),
+                in1=b3bc[:, hs].unsqueeze(2).to_broadcast([P, DK, 4]),
+                op=ALU.add,
+            )
+
+        def quantise_imf(g):
             nc.vector.quantize_mx(
                 out=ic[:, g, :].bitcast(FP8X4),
                 scales=isc[:, g, :],
                 in_=ig[:, g, :, :].rearrange("p o t -> p (o t)"),
             )
+
+        side = [
+            [(prep_q, (0, 1))],
+            [(words_to_k_on_partitions, (x_raw, xg, 0))],
+            [(words_to_k_on_partitions, (x_raw, xg, 1))],
+            [(words_to_k_on_partitions, (x_raw, xg, 2)), (quantise_x, (0,))],
+            [(words_to_k_on_partitions, (x_raw, xg, 3))],
+            [(words_to_k_on_partitions, (w_raw, wg, 0)), (quantise_x, (1,))],
+            [(words_to_k_on_partitions, (w_raw, wg, 1)), (quantise_w, ())],
+            [(project, (0, 0))],
+            [(prep_q, (0, 2))],
+            [(project, (0, 1))],
+            [(project, (0, 2))],
+            [(project, (0, 3))],
+            [(project, (1, 0)), (quantise_imf, (0,))],
+            [(prep_q, (0, 3))],
+            [(project, (1, 1))],
+            [(project, (1, 2))],
+            [(project, (1, 3)), (quantise_imf, (1,))],
+        ]
 
         s_t, nb_t, e_t, et_t, eg_t, ec_t, es_t, rs_t, pv_t = {}, {}, {}, {}, {}, {}, {}, {}, {}
 
@@ -182,7 +208,7 @@ def tile_multiheadedattention_pa_t_kernel(tc, q, k, image_feat, W3, b3, out):
 
         def exponent(i):
             if i % GRP == 0:
-                rs_t[i // GRP] = stat.tile([P, GRP, 2], F32, name="rs", tag="rs")
+                rs_t[i // GRP] = sums.tile([P, GRP, 2], F32, name="rs", tag="rs")
             rs = rs_t[i // GRP]
             e = work.tile([P, SK], BF16, name="e", tag="e")
             for c in range(2):
@@ -205,15 +231,15 @@ def tile_multiheadedattention_pa_t_kernel(tc, q, k, image_feat, W3, b3, out):
         def regroup(i):
             eg = work.tile([P, 2, P, 4], BF16, name="eg", tag="eg", align_bytes=64)
             src = et_t[i][:].rearrange("p (g t) r -> p g r t", g=2)
-            if i % DVE_COPY_EVERY == DVE_COPY_EVERY - 1:
+            if i >= len(side) and i % 4 == 3:
                 nc.vector.tensor_copy(out=eg[:], in_=src)
             else:
                 nc.scalar.copy(out=eg[:], in_=src)
             eg_t[i] = eg
 
         def quantise(i):
-            ec = work.tile([P, 2 * P], U32, name="ec", tag="ec", align_bytes=64)
-            es = work.tile([P, 2 * P], U8, name="es", tag="es", align_bytes=64)
+            ec = codes.tile([P, 2 * P], U32, name="ec", tag="ec", align_bytes=64)
+            es = codes.tile([P, 2 * P], U8, name="es", tag="es", align_bytes=64)
             nc.vector.quantize_mx(
                 out=ec[:].bitcast(FP8X4),
                 scales=es[:],
@@ -263,11 +289,13 @@ def tile_multiheadedattention_pa_t_kernel(tc, q, k, image_feat, W3, b3, out):
         def live(i):
             return 0 <= i < NT
 
-        if PIN:
-            ctx.enter_context(tc.manual_schedule())
-        for step in range(-1, NT + 2):
-            if live(step - 2):
-                quantise(step - 2)
+        ctx.enter_context(tc.manual_schedule())
+        prep_k(0)
+        prep_q(0, 0)
+        pooled = {"n": 0}
+        for step in range(-1, NT + QLAG):
+            if live(step - QLAG):
+                quantise(step - QLAG)
             if live(step + 1):
                 scores(step + 1)
                 row_max(step + 1)
@@ -276,14 +304,21 @@ def tile_multiheadedattention_pa_t_kernel(tc, q, k, image_feat, W3, b3, out):
             if live(step - 1):
                 flip(step - 1)
                 regroup(step - 1)
-            if live(step - 2):
-                pool_features(step - 2)
-                if (step - 2) % GRP == GRP - 1:
-                    finish((step - 2) // GRP)
+            if step >= len(side):
+                for rep in range(2):
+                    i = pooled["n"]
+                    if i < NT and i <= step - QLAG:
+                        pool_features(i)
+                        if i % GRP == GRP - 1:
+                            finish(i // GRP)
+                        pooled["n"] = i + 1
+            if 0 <= step < len(side):
+                for fn, args in side[step]:
+                    fn(*args)
             if live(step):
                 h, n = divmod(step, NQ)
                 if h + 1 < H:
-                    if n == 8:
+                    if n == 18:
                         prep_k(h + 1)
-                    if n in (12, 16, 20, 24):
-                        prep_q(h + 1, (n - 12) // 4)
+                    if n in (20, 22, 24, 26):
+                        prep_q(h + 1, (n - 20) // 2)

@@ -22,8 +22,9 @@ NB = SK // P
 GRP = 4
 SCALE = 1.0 / math.sqrt(DK)
 FLOPS = 2 * SK * D * D + 2 * 2 * H * SQ * SK * DK
-QLAG = 3
 EC_BUFS = 20
+X0, W0, I0, PV0 = 2, 6, 9, 18
+QV = 48
 
 
 def tile_multiheadedattention_pa_t_kernel(tc, q, k, image_feat, W3, b3, out):
@@ -37,7 +38,7 @@ def tile_multiheadedattention_pa_t_kernel(tc, q, k, image_feat, W3, b3, out):
         const = ctx.enter_context(tc.tile_pool(name="const", bufs=1))
         qraw_pool = ctx.enter_context(tc.tile_pool(name="qraw", bufs=H))
         qt_pool = ctx.enter_context(tc.tile_pool(name="qt", bufs=2))
-        work = ctx.enter_context(tc.tile_pool(name="work", bufs=4))
+        work = ctx.enter_context(tc.tile_pool(name="work", bufs=5))
         codes = ctx.enter_context(tc.tile_pool(name="codes", bufs=EC_BUFS))
         stat = ctx.enter_context(tc.tile_pool(name="stat", bufs=4))
         sums = ctx.enter_context(tc.tile_pool(name="sums", bufs=8))
@@ -109,7 +110,7 @@ def tile_multiheadedattention_pa_t_kernel(tc, q, k, image_feat, W3, b3, out):
         def words_to_k_on_partitions(raw, grouped, pair):
             raw32 = raw[:].bitcast(F32)
             grouped32 = grouped[:].bitcast(F32)
-            px = ps_p.tile([P, 2, 2, P], F32, name="px", tag="prep")
+            px = ps_o.tile([P, 2, 2, P], F32, name="px", tag="pv")
             for a in range(2):
                 for u in range(2):
                     c0 = (2 * pair + a) * (D // 2) + u * P
@@ -133,7 +134,7 @@ def tile_multiheadedattention_pa_t_kernel(tc, q, k, image_feat, W3, b3, out):
 
         def project(g, h):
             hs = slice(h * DK, (h + 1) * DK)
-            pi = ps_p.tile([P, 4, DK], F32, name="pi", tag="prep")
+            pi = ps_o.tile([P, 4, DK], F32, name="pi", tag="pv")
             for t in range(4):
                 bs = slice((4 * g + t) * P, (4 * g + t + 1) * P)
                 nc.tensor.matmul_mx(
@@ -159,27 +160,8 @@ def tile_multiheadedattention_pa_t_kernel(tc, q, k, image_feat, W3, b3, out):
                 in_=ig[:, g, :, :].rearrange("p o t -> p (o t)"),
             )
 
-        side = [
-            [(prep_q, (0, 1))],
-            [(words_to_k_on_partitions, (x_raw, xg, 0))],
-            [(words_to_k_on_partitions, (x_raw, xg, 1))],
-            [(words_to_k_on_partitions, (x_raw, xg, 2)), (quantise_x, (0,))],
-            [(words_to_k_on_partitions, (x_raw, xg, 3))],
-            [(words_to_k_on_partitions, (w_raw, wg, 0)), (quantise_x, (1,))],
-            [(words_to_k_on_partitions, (w_raw, wg, 1)), (quantise_w, ())],
-            [(project, (0, 0))],
-            [(prep_q, (0, 2))],
-            [(project, (0, 1))],
-            [(project, (0, 2))],
-            [(project, (0, 3))],
-            [(project, (1, 0)), (quantise_imf, (0,))],
-            [(prep_q, (0, 3))],
-            [(project, (1, 1))],
-            [(project, (1, 2))],
-            [(project, (1, 3)), (quantise_imf, (1,))],
-        ]
-
         s_t, nb_t, e_t, et_t, eg_t, ec_t, es_t, rs_t, pv_t = {}, {}, {}, {}, {}, {}, {}, {}, {}
+        rsum_t, rcp_t, mx_t = {}, {}, {}
 
         def scores(i):
             h, n = divmod(i, NQ)
@@ -200,6 +182,10 @@ def tile_multiheadedattention_pa_t_kernel(tc, q, k, image_feat, W3, b3, out):
             mx = stat.tile([P, 2], F32, name="mx", tag="mx")
             for c in range(2):
                 nc.vector.tensor_reduce(out=mx[:, c : c + 1], in_=s_t[i][c][:], axis=AX.X, op=ALU.max)
+            mx_t[i] = mx
+
+        def shift(i):
+            mx = mx_t[i]
             nb = stat.tile([P, 1], F32, name="nb", tag="nb")
             nc.vector.tensor_scalar(
                 out=nb[:], in0=mx[:, 0:1], scalar1=mx[:, 1:2], scalar2=-SCALE, op0=ALU.max, op1=ALU.mult
@@ -228,14 +214,15 @@ def tile_multiheadedattention_pa_t_kernel(tc, q, k, image_feat, W3, b3, out):
                 nc.tensor.transpose(et[:, b, :], e_t[i][:, b * P : (b + 1) * P], ident_b[:])
             et_t[i] = et
 
-        def regroup(i):
-            eg = work.tile([P, 2, P, 4], BF16, name="eg", tag="eg", align_bytes=64)
-            src = et_t[i][:].rearrange("p (g t) r -> p g r t", g=2)
-            if i >= len(side) and i % 4 == 3:
-                nc.vector.tensor_copy(out=eg[:], in_=src)
+        def regroup(i, on_vector, lo, hi):
+            if i not in eg_t:
+                eg_t[i] = work.tile([P, 2, P, 4], BF16, name="eg", tag="eg", align_bytes=64)
+            dst = eg_t[i][:, :, lo:hi, :]
+            src = et_t[i][:, :, lo:hi].rearrange("p (g t) r -> p g r t", g=2)
+            if on_vector:
+                nc.vector.tensor_copy(out=dst, in_=src)
             else:
-                nc.scalar.copy(out=eg[:], in_=src)
-            eg_t[i] = eg
+                nc.scalar.copy(out=dst, in_=src)
 
         def quantise(i):
             ec = codes.tile([P, 2 * P], U32, name="ec", tag="ec", align_bytes=64)
@@ -266,12 +253,19 @@ def tile_multiheadedattention_pa_t_kernel(tc, q, k, image_feat, W3, b3, out):
                     stop=(g == 1),
                 )
 
+        def row_sum(grp):
+            rsum = sums.tile([P, GRP], F32, name="rsum", tag="rsum")
+            nc.vector.tensor_tensor(out=rsum[:], in0=rs_t[grp][:, :, 0], in1=rs_t[grp][:, :, 1], op=ALU.add)
+            rsum_t[grp] = rsum
+
+        def invert(grp):
+            rcp = sums.tile([P, GRP], F32, name="rcp", tag="rcp")
+            nc.vector.reciprocal(out=rcp[:], in_=rsum_t[grp][:])
+            rcp_t[grp] = rcp
+
         def finish(grp):
             h, m = divmod(grp, NQ // GRP)
-            rsum = stat.tile([P, GRP], F32, name="rsum", tag="rsum")
-            nc.vector.tensor_reduce(out=rsum[:], in_=rs_t[grp][:], axis=AX.X, op=ALU.add)
-            rcp = stat.tile([P, GRP], F32, name="rcp", tag="rcp")
-            nc.vector.reciprocal(out=rcp[:], in_=rsum[:])
+            rcp = rcp_t[grp]
             o_sb = work.tile([P, GRP, DK], F32, name="o_sb", tag="o_sb")
             nc.vector.tensor_tensor(
                 out=o_sb[:],
@@ -292,33 +286,52 @@ def tile_multiheadedattention_pa_t_kernel(tc, q, k, image_feat, W3, b3, out):
         ctx.enter_context(tc.manual_schedule())
         prep_k(0)
         prep_q(0, 0)
-        pooled = {"n": 0}
-        for step in range(-1, NT + QLAG):
-            if live(step - QLAG):
-                quantise(step - QLAG)
+        pooled = {"tiles": 0, "groups": 0}
+        for step in range(-1, NT + 6):
+            emptying = pooled["tiles"] >= GRP * (pooled["groups"] + 1)
+            if emptying:
+                finish(pooled["groups"])
+                pooled["groups"] = pooled["groups"] + 1
+            qv = 0 if (emptying or step < PV0) else QV
+            if live(step - 2) and qv > 0:
+                regroup(step - 2, True, 0, qv)
             if live(step + 1):
                 scores(step + 1)
                 row_max(step + 1)
+            if live(step - 3):
+                quantise(step - 3)
+            if live(step + 1):
+                shift(step + 1)
             if live(step):
                 exponent(step)
             if live(step - 1):
                 flip(step - 1)
-                regroup(step - 1)
-            if step >= len(side):
+                if (step - 1) % GRP == GRP - 1:
+                    row_sum((step - 1) // GRP)
+            if live(step - 2):
+                if (step - 2) % GRP == GRP - 1:
+                    invert((step - 2) // GRP)
+                regroup(step - 2, False, qv, P)
+            if step >= PV0:
                 for rep in range(2):
-                    i = pooled["n"]
-                    if i < NT and i <= step - QLAG:
+                    i = pooled["tiles"]
+                    if i < NT and i <= step - 4:
                         pool_features(i)
-                        if i % GRP == GRP - 1:
-                            finish(i // GRP)
-                        pooled["n"] = i + 1
-            if 0 <= step < len(side):
-                for fn, args in side[step]:
-                    fn(*args)
-            if live(step):
-                h, n = divmod(step, NQ)
-                if h + 1 < H:
-                    if n == 18:
-                        prep_k(h + 1)
-                    if n in (20, 22, 24, 26):
-                        prep_q(h + 1, (n - 20) // 2)
+                        pooled["tiles"] = i + 1
+            if X0 <= step < X0 + 4:
+                words_to_k_on_partitions(x_raw, xg, step - X0)
+            if step in (X0 + 2, X0 + 4):
+                quantise_x((step - X0) // 2 - 1)
+            if W0 <= step < W0 + 2:
+                words_to_k_on_partitions(w_raw, wg, step - W0)
+            if step == W0 + 2:
+                quantise_w()
+            if I0 <= step < I0 + 8:
+                project((step - I0) // 4, (step - I0) % 4)
+            if step in (I0 + 4, I0 + 8):
+                quantise_imf((step - I0) // 4 - 1)
+            h, n = divmod(step + 6, NQ)
+            if 0 < step + 6 < NT and n % 8 == 0:
+                prep_q(h, n // 8)
+            if 0 < step + 8 < NT and (step + 8) % NQ == 0:
+                prep_k((step + 8) // NQ)

@@ -24,7 +24,7 @@ SCALE = 1.0 / math.sqrt(DK)
 FLOPS = 2 * SK * D * D + 2 * 2 * H * SQ * SK * DK
 EC_BUFS = 20
 X0, W0, I0, PV0 = 2, 6, 9, 18
-QV = 48
+QV = 16
 
 
 def tile_multiheadedattention_pa_t_kernel(tc, q, k, image_feat, W3, b3, out):
@@ -42,6 +42,7 @@ def tile_multiheadedattention_pa_t_kernel(tc, q, k, image_feat, W3, b3, out):
         codes = ctx.enter_context(tc.tile_pool(name="codes", bufs=EC_BUFS))
         stat = ctx.enter_context(tc.tile_pool(name="stat", bufs=4))
         sums = ctx.enter_context(tc.tile_pool(name="sums", bufs=8))
+        lone = ctx.enter_context(tc.tile_pool(name="lone", bufs=1))
         ps_s = ctx.enter_context(tc.psum_pool(name="ps_s", bufs=4))
         ps_t = ctx.enter_context(tc.psum_pool(name="ps_t", bufs=2))
         ps_o = ctx.enter_context(tc.psum_pool(name="ps_o", bufs=1))
@@ -161,7 +162,7 @@ def tile_multiheadedattention_pa_t_kernel(tc, q, k, image_feat, W3, b3, out):
             )
 
         s_t, nb_t, e_t, et_t, eg_t, ec_t, es_t, rs_t, pv_t = {}, {}, {}, {}, {}, {}, {}, {}, {}
-        rsum_t, rcp_t, mx_t = {}, {}, {}
+        rsum_t, rcp_t, mx_t, ep_t, eh_t = {}, {}, {}, {}, {}
 
         def scores(i):
             h, n = divmod(i, NQ)
@@ -216,22 +217,40 @@ def tile_multiheadedattention_pa_t_kernel(tc, q, k, image_feat, W3, b3, out):
 
         def regroup(i, on_vector, lo, hi):
             if i not in eg_t:
-                eg_t[i] = work.tile([P, 2, P, 4], BF16, name="eg", tag="eg", align_bytes=64)
-            dst = eg_t[i][:, :, lo:hi, :]
-            src = et_t[i][:, :, lo:hi].rearrange("p (g t) r -> p g r t", g=2)
+                eg_t[i] = work.tile([P, P, 4], BF16, name="eg", tag="eg", align_bytes=64)
+            dst = eg_t[i][:, lo:hi, :]
+            src = et_t[i][:, 0:4, lo:hi].rearrange("p t r -> p r t")
             if on_vector:
                 nc.vector.tensor_copy(out=dst, in_=src)
             else:
                 nc.scalar.copy(out=dst, in_=src)
 
+        def planes(i):
+            ep = work.tile([P, 4, P], BF16, name="ep", tag="ep")
+            nc.scalar.copy(out=ep[:], in_=et_t[i][:, 4:8, :])
+            ep_t[i] = ep
+
+        def regroup_late(i):
+            eh = lone.tile([P, P, 4], BF16, name="eh", tag="eh", align_bytes=64)
+            nc.gpsimd.tensor_scalar(
+                out=eh[:],
+                in0=ep_t[i][:].rearrange("p t r -> p r t"),
+                scalar1=1.0,
+                scalar2=0.0,
+                op0=ALU.mult,
+                op1=ALU.add,
+            )
+            eh_t[i] = eh
+
         def quantise(i):
             ec = codes.tile([P, 2 * P], U32, name="ec", tag="ec", align_bytes=64)
             es = codes.tile([P, 2 * P], U8, name="es", tag="es", align_bytes=64)
-            nc.vector.quantize_mx(
-                out=ec[:].bitcast(FP8X4),
-                scales=es[:],
-                in_=eg_t[i][:].rearrange("p g r t -> p (g r t)"),
-            )
+            for g, grouped in enumerate((eg_t[i], eh_t[i])):
+                nc.vector.quantize_mx(
+                    out=ec[:, g * P : (g + 1) * P].bitcast(FP8X4),
+                    scales=es[:, g * P : (g + 1) * P],
+                    in_=grouped[:].rearrange("p r t -> p (r t)"),
+                )
             ec_t[i] = ec
             es_t[i] = es
 
@@ -287,7 +306,10 @@ def tile_multiheadedattention_pa_t_kernel(tc, q, k, image_feat, W3, b3, out):
         prep_k(0)
         prep_q(0, 0)
         pooled = {"tiles": 0, "groups": 0}
-        for step in range(-1, NT + 6):
+        for step in range(-1, NT + 7):
+            if live(step + 1):
+                scores(step + 1)
+                row_max(step + 1)
             emptying = pooled["tiles"] >= GRP * (pooled["groups"] + 1)
             if emptying:
                 finish(pooled["groups"])
@@ -295,27 +317,27 @@ def tile_multiheadedattention_pa_t_kernel(tc, q, k, image_feat, W3, b3, out):
             qv = 0 if (emptying or step < PV0) else QV
             if live(step - 2) and qv > 0:
                 regroup(step - 2, True, 0, qv)
-            if live(step + 1):
-                scores(step + 1)
-                row_max(step + 1)
-            if live(step - 3):
-                quantise(step - 3)
+            if live(step - 1) and (step - 1) % GRP == GRP - 1:
+                row_sum((step - 1) // GRP)
+            if live(step - 2) and (step - 2) % GRP == GRP - 1:
+                invert((step - 2) // GRP)
             if live(step + 1):
                 shift(step + 1)
+            if live(step - 4):
+                quantise(step - 4)
+            if live(step - 3):
+                regroup_late(step - 3)
             if live(step):
                 exponent(step)
             if live(step - 1):
                 flip(step - 1)
-                if (step - 1) % GRP == GRP - 1:
-                    row_sum((step - 1) // GRP)
             if live(step - 2):
-                if (step - 2) % GRP == GRP - 1:
-                    invert((step - 2) // GRP)
+                planes(step - 2)
                 regroup(step - 2, False, qv, P)
             if step >= PV0:
                 for rep in range(2):
                     i = pooled["tiles"]
-                    if i < NT and i <= step - 4:
+                    if i < NT and i <= step - 5:
                         pool_features(i)
                         pooled["tiles"] = i + 1
             if X0 <= step < X0 + 4:

@@ -24,7 +24,6 @@ SCALE = 1.0 / math.sqrt(DK)
 FLOPS = 2 * SK * D * D + 2 * 2 * H * SQ * SK * DK
 EC_BUFS = 20
 X0, W0, I0, PV0 = 2, 6, 9, 18
-QV = 16
 
 
 def tile_multiheadedattention_pa_t_kernel(tc, q, k, image_feat, W3, b3, out):
@@ -42,7 +41,7 @@ def tile_multiheadedattention_pa_t_kernel(tc, q, k, image_feat, W3, b3, out):
         codes = ctx.enter_context(tc.tile_pool(name="codes", bufs=EC_BUFS))
         stat = ctx.enter_context(tc.tile_pool(name="stat", bufs=4))
         sums = ctx.enter_context(tc.tile_pool(name="sums", bufs=8))
-        lone = ctx.enter_context(tc.tile_pool(name="lone", bufs=1))
+        lone = ctx.enter_context(tc.tile_pool(name="lone", bufs=3))
         ps_s = ctx.enter_context(tc.psum_pool(name="ps_s", bufs=4))
         ps_t = ctx.enter_context(tc.psum_pool(name="ps_t", bufs=2))
         ps_o = ctx.enter_context(tc.psum_pool(name="ps_o", bufs=1))
@@ -215,19 +214,17 @@ def tile_multiheadedattention_pa_t_kernel(tc, q, k, image_feat, W3, b3, out):
                 nc.tensor.transpose(et[:, b, :], e_t[i][:, b * P : (b + 1) * P], ident_b[:])
             et_t[i] = et
 
-        def regroup(i, on_vector, lo, hi):
-            if i not in eg_t:
-                eg_t[i] = work.tile([P, P, 4], BF16, name="eg", tag="eg", align_bytes=64)
-            dst = eg_t[i][:, lo:hi, :]
-            src = et_t[i][:, 0:4, lo:hi].rearrange("p t r -> p r t")
-            if on_vector:
-                nc.vector.tensor_copy(out=dst, in_=src)
-            else:
-                nc.scalar.copy(out=dst, in_=src)
+        def regroup(i):
+            eg = work.tile([P, P, 4], BF16, name="eg", tag="eg", align_bytes=64)
+            nc.scalar.copy(out=eg[:], in_=et_t[i][:, 0:4, :].rearrange("p t r -> p r t"))
+            eg_t[i] = eg
 
-        def planes(i):
+        def planes(i, on_vector):
             ep = work.tile([P, 4, P], BF16, name="ep", tag="ep")
-            nc.scalar.copy(out=ep[:], in_=et_t[i][:, 4:8, :])
+            if on_vector:
+                nc.vector.tensor_copy(out=ep[:], in_=et_t[i][:, 4:8, :])
+            else:
+                nc.scalar.copy(out=ep[:], in_=et_t[i][:, 4:8, :])
             ep_t[i] = ep
 
         def regroup_late(i):
@@ -307,24 +304,24 @@ def tile_multiheadedattention_pa_t_kernel(tc, q, k, image_feat, W3, b3, out):
         prep_q(0, 0)
         pooled = {"tiles": 0, "groups": 0}
         for step in range(-1, NT + 7):
-            if live(step + 1):
-                scores(step + 1)
-                row_max(step + 1)
             emptying = pooled["tiles"] >= GRP * (pooled["groups"] + 1)
             if emptying:
                 finish(pooled["groups"])
                 pooled["groups"] = pooled["groups"] + 1
-            qv = 0 if (emptying or step < PV0) else QV
-            if live(step - 2) and qv > 0:
-                regroup(step - 2, True, 0, qv)
+            vector_has_room = not (emptying or step < PV0)
+            if live(step - 2) and vector_has_room:
+                planes(step - 2, True)
+            if live(step + 1):
+                scores(step + 1)
+                row_max(step + 1)
+            if live(step - 4):
+                quantise(step - 4)
+            if live(step + 1):
+                shift(step + 1)
             if live(step - 1) and (step - 1) % GRP == GRP - 1:
                 row_sum((step - 1) // GRP)
             if live(step - 2) and (step - 2) % GRP == GRP - 1:
                 invert((step - 2) // GRP)
-            if live(step + 1):
-                shift(step + 1)
-            if live(step - 4):
-                quantise(step - 4)
             if live(step - 3):
                 regroup_late(step - 3)
             if live(step):
@@ -332,8 +329,9 @@ def tile_multiheadedattention_pa_t_kernel(tc, q, k, image_feat, W3, b3, out):
             if live(step - 1):
                 flip(step - 1)
             if live(step - 2):
-                planes(step - 2)
-                regroup(step - 2, False, qv, P)
+                if not vector_has_room:
+                    planes(step - 2, False)
+                regroup(step - 2)
             if step >= PV0:
                 for rep in range(2):
                     i = pooled["tiles"]

@@ -41,7 +41,6 @@ def tile_multiheadedattention_pa_t_kernel(tc, q, k, image_feat, W3, b3, out):
         codes = ctx.enter_context(tc.tile_pool(name="codes", bufs=EC_BUFS))
         stat = ctx.enter_context(tc.tile_pool(name="stat", bufs=4))
         sums = ctx.enter_context(tc.tile_pool(name="sums", bufs=8))
-        lone = ctx.enter_context(tc.tile_pool(name="lone", bufs=3))
         ps_s = ctx.enter_context(tc.psum_pool(name="ps_s", bufs=4))
         ps_t = ctx.enter_context(tc.psum_pool(name="ps_t", bufs=2))
         ps_o = ctx.enter_context(tc.psum_pool(name="ps_o", bufs=1))
@@ -59,15 +58,18 @@ def tile_multiheadedattention_pa_t_kernel(tc, q, k, image_feat, W3, b3, out):
         q_raws = []
         for h in range(H):
             nc.sync.dma_start(
-                out=k_raw[:, h, :, :],
-                in_=kf[h * SK : (h + 1) * SK, :].rearrange("(p n) d -> p n d", n=NB),
+                out=k_raw[:, h, :, :].rearrange("p (g t) d -> p g (t d)", g=2),
+                in_=kf[h * SK : (h + 1) * SK, :].rearrange("(g p t) d -> p g (t d)", g=2, t=4),
             )
             q_raw = qraw_pool.tile([P, NQ, DK], BF16, name="q_raw", tag="q_raw")
             q_src = qf[h * SQ : (h + 1) * SQ, :].rearrange("(p n) d -> p n d", n=NQ)
             if h == 0:
                 for r in range(2):
                     nc.sync.dma_start(out=q_raw[:, 8 * r : 8 * r + 8, :], in_=q_src[:, 8 * r : 8 * r + 8, :])
-                nc.sync.dma_start(out=x_raw[:], in_=xf.rearrange("(p n) c -> p (n c)", n=NB))
+                nc.sync.dma_start(
+                    out=x_raw[:].rearrange("p (g w) -> p g w", g=2),
+                    in_=xf.rearrange("(g p t) c -> p g (t c)", g=2, t=4),
+                )
                 nc.sync.dma_start(
                     out=w_raw[:].rearrange("p (n c) -> p n c", n=H),
                     in_=W3.rearrange("(n p) c -> p n c", p=P),
@@ -86,7 +88,8 @@ def tile_multiheadedattention_pa_t_kernel(tc, q, k, image_feat, W3, b3, out):
             for n in range(NB):
                 nc.tensor.transpose(pk[:, n, :], k_raw[:, h, n, :], ident_b[:])
             nc.vector.tensor_copy(
-                out=kT[:, h, :].rearrange("p (n r) -> p n r", n=NB), in_=pk[:]
+                out=kT[:, h, :].rearrange("p (a r e) -> p a r e", a=4, e=2),
+                in_=pk[:].rearrange("p (a e) r -> p a r e", e=2),
             )
 
         def prep_q(h, r):
@@ -161,7 +164,7 @@ def tile_multiheadedattention_pa_t_kernel(tc, q, k, image_feat, W3, b3, out):
             )
 
         s_t, nb_t, e_t, et_t, eg_t, ec_t, es_t, rs_t, pv_t = {}, {}, {}, {}, {}, {}, {}, {}, {}
-        rsum_t, rcp_t, mx_t, ep_t, eh_t = {}, {}, {}, {}, {}
+        rsum_t, rcp_t, mx_t = {}, {}, {}
 
         def scores(i):
             h, n = divmod(i, NQ)
@@ -209,45 +212,24 @@ def tile_multiheadedattention_pa_t_kernel(tc, q, k, image_feat, W3, b3, out):
             e_t[i] = e
 
         def flip(i):
-            et = ps_t.tile([P, NB, P], BF16, name="et", tag="et")
-            for b in range(NB):
-                nc.tensor.transpose(et[:, b, :], e_t[i][:, b * P : (b + 1) * P], ident_b[:])
+            words = e_t[i][:].bitcast(F32)
+            et = ps_t.tile([P, 4, P], F32, name="et", tag="et")
+            for m in range(4):
+                nc.tensor.transpose(et[:, m, :], words[:, m * P : (m + 1) * P], ident_f[:])
             et_t[i] = et
 
         def regroup(i):
-            eg = work.tile([P, P, 4], BF16, name="eg", tag="eg", align_bytes=64)
-            nc.scalar.copy(out=eg[:], in_=et_t[i][:, 0:4, :].rearrange("p t r -> p r t"))
-            eg_t[i] = eg
-
-        def planes(i, on_vector):
-            ep = work.tile([P, 4, P], BF16, name="ep", tag="ep")
-            if on_vector:
-                nc.vector.tensor_copy(out=ep[:], in_=et_t[i][:, 4:8, :])
-            else:
-                nc.scalar.copy(out=ep[:], in_=et_t[i][:, 4:8, :])
-            ep_t[i] = ep
-
-        def regroup_late(i):
-            eh = lone.tile([P, P, 4], BF16, name="eh", tag="eh", align_bytes=64)
-            nc.gpsimd.tensor_scalar(
-                out=eh[:],
-                in0=ep_t[i][:].rearrange("p t r -> p r t"),
-                scalar1=1.0,
-                scalar2=0.0,
-                op0=ALU.mult,
-                op1=ALU.add,
+            eg = work.tile([P, SK], BF16, name="eg", tag="eg", align_bytes=64)
+            nc.scalar.copy(
+                out=eg[:].bitcast(F32).rearrange("p (g r u) -> p g r u", g=2, u=2),
+                in_=et_t[i][:].rearrange("p (g u) r -> p g r u", g=2),
             )
-            eh_t[i] = eh
+            eg_t[i] = eg
 
         def quantise(i):
             ec = codes.tile([P, 2 * P], U32, name="ec", tag="ec", align_bytes=64)
             es = codes.tile([P, 2 * P], U8, name="es", tag="es", align_bytes=64)
-            for g, grouped in enumerate((eg_t[i], eh_t[i])):
-                nc.vector.quantize_mx(
-                    out=ec[:, g * P : (g + 1) * P].bitcast(FP8X4),
-                    scales=es[:, g * P : (g + 1) * P],
-                    in_=grouped[:].rearrange("p r t -> p (r t)"),
-                )
+            nc.vector.quantize_mx(out=ec[:].bitcast(FP8X4), scales=es[:], in_=eg_t[i][:])
             ec_t[i] = ec
             es_t[i] = es
 
@@ -308,34 +290,27 @@ def tile_multiheadedattention_pa_t_kernel(tc, q, k, image_feat, W3, b3, out):
             if emptying:
                 finish(pooled["groups"])
                 pooled["groups"] = pooled["groups"] + 1
-            vector_has_room = not (emptying or step < PV0)
-            if live(step - 2) and vector_has_room:
-                planes(step - 2, True)
             if live(step + 1):
                 scores(step + 1)
                 row_max(step + 1)
-            if live(step - 4):
-                quantise(step - 4)
+            if live(step - 3):
+                quantise(step - 3)
             if live(step + 1):
                 shift(step + 1)
             if live(step - 1) and (step - 1) % GRP == GRP - 1:
                 row_sum((step - 1) // GRP)
             if live(step - 2) and (step - 2) % GRP == GRP - 1:
                 invert((step - 2) // GRP)
-            if live(step - 3):
-                regroup_late(step - 3)
             if live(step):
                 exponent(step)
             if live(step - 1):
                 flip(step - 1)
             if live(step - 2):
-                if not vector_has_room:
-                    planes(step - 2, False)
                 regroup(step - 2)
             if step >= PV0:
                 for rep in range(2):
                     i = pooled["tiles"]
-                    if i < NT and i <= step - 5:
+                    if i < NT and i <= step - 4:
                         pool_features(i)
                         pooled["tiles"] = i + 1
             if X0 <= step < X0 + 4:

@@ -23,7 +23,8 @@ GRP = 4
 SCALE = 1.0 / math.sqrt(DK)
 FLOPS = 2 * SK * D * D + 2 * 2 * H * SQ * SK * DK
 EC_BUFS = 20
-X0, W0, I0, PV0 = 2, 6, 9, 18
+X0, W0, I0, PV0 = 2, 6, 9, 19
+LEAD = 2
 
 
 def tile_multiheadedattention_pa_t_kernel(tc, q, k, image_feat, W3, b3, out):
@@ -41,10 +42,9 @@ def tile_multiheadedattention_pa_t_kernel(tc, q, k, image_feat, W3, b3, out):
         codes = ctx.enter_context(tc.tile_pool(name="codes", bufs=EC_BUFS))
         stat = ctx.enter_context(tc.tile_pool(name="stat", bufs=4))
         sums = ctx.enter_context(tc.tile_pool(name="sums", bufs=8))
-        ps_s = ctx.enter_context(tc.psum_pool(name="ps_s", bufs=4))
-        ps_t = ctx.enter_context(tc.psum_pool(name="ps_t", bufs=2))
+        ps_s = ctx.enter_context(tc.psum_pool(name="ps_s", bufs=6))
+        ps_t = ctx.enter_context(tc.psum_pool(name="ps_t", bufs=1))
         ps_o = ctx.enter_context(tc.psum_pool(name="ps_o", bufs=1))
-        ps_p = ctx.enter_context(tc.psum_pool(name="ps_p", bufs=1))
 
         ident_b = const.tile([P, P], BF16, name="ident_b")
         make_identity(nc, ident_b[:])
@@ -83,8 +83,8 @@ def tile_multiheadedattention_pa_t_kernel(tc, q, k, image_feat, W3, b3, out):
         kT = const.tile([P, H, SK], BF16, name="kT")
         qTs = {}
 
-        def prep_k(h):
-            pk = ps_p.tile([P, NB, P], BF16, name="pk", tag="prep")
+        def prep_k(h, bank, tag):
+            pk = bank.tile([P, NB, P], BF16, name="pk", tag=tag)
             for n in range(NB):
                 nc.tensor.transpose(pk[:, n, :], k_raw[:, h, n, :], ident_b[:])
             nc.vector.tensor_copy(
@@ -95,7 +95,7 @@ def tile_multiheadedattention_pa_t_kernel(tc, q, k, image_feat, W3, b3, out):
         def prep_q(h, r):
             if r == 0:
                 qTs[h] = qt_pool.tile([P, NQ, P], BF16, name="qT", tag="qT")
-            pq = ps_p.tile([P, 8, P], BF16, name="pq", tag="prep")
+            pq = ps_o.tile([P, 8, P], BF16, name="pq", tag="pv")
             for a in range(8):
                 nc.tensor.transpose(pq[:, a, :], q_raws[h][:, 8 * r + a, :], ident_b[:])
             nc.vector.tensor_copy(out=qTs[h][:, 8 * r : 8 * r + 8, :], in_=pq[:])
@@ -282,21 +282,21 @@ def tile_multiheadedattention_pa_t_kernel(tc, q, k, image_feat, W3, b3, out):
             return 0 <= i < NT
 
         ctx.enter_context(tc.manual_schedule())
-        prep_k(0)
+        prep_k(0, ps_t, "et")
         prep_q(0, 0)
         pooled = {"tiles": 0, "groups": 0}
-        for step in range(-1, NT + 7):
-            emptying = pooled["tiles"] >= GRP * (pooled["groups"] + 1)
-            if emptying:
-                finish(pooled["groups"])
-                pooled["groups"] = pooled["groups"] + 1
-            if live(step + 1):
-                scores(step + 1)
-                row_max(step + 1)
+        for step in range(-LEAD, NT + 7):
+            ahead = step + LEAD
+            if live(ahead):
+                scores(ahead)
+                row_max(ahead)
             if live(step - 3):
                 quantise(step - 3)
-            if live(step + 1):
-                shift(step + 1)
+            if live(ahead):
+                shift(ahead)
+            if pooled["tiles"] >= GRP * (pooled["groups"] + 1):
+                finish(pooled["groups"])
+                pooled["groups"] = pooled["groups"] + 1
             if live(step - 1) and (step - 1) % GRP == GRP - 1:
                 row_sum((step - 1) // GRP)
             if live(step - 2) and (step - 2) % GRP == GRP - 1:
@@ -305,12 +305,16 @@ def tile_multiheadedattention_pa_t_kernel(tc, q, k, image_feat, W3, b3, out):
                 exponent(step)
             if live(step - 1):
                 flip(step - 1)
-            if live(step - 2):
-                regroup(step - 2)
-            if step >= PV0:
-                for rep in range(2):
-                    i = pooled["tiles"]
-                    if i < NT and i <= step - 4:
+                regroup(step - 1)
+            h, n = divmod(step + 7, NQ)
+            if 0 < step + 7 < NT and n % 8 == 0:
+                prep_q(h, n // 8)
+            if 0 < step + 8 < NT and (step + 8) % NQ == 0:
+                prep_k((step + 8) // NQ, ps_o, "pv")
+            if step >= PV0 and pooled["tiles"] == GRP * pooled["groups"] or pooled["tiles"] >= NT - GRP:
+                end = min(pooled["tiles"] - pooled["tiles"] % GRP + GRP, NT)
+                if end == NT or end <= step - 3 and step % 2 == 1:
+                    for i in range(pooled["tiles"], min(end, step - 3)):
                         pool_features(i)
                         pooled["tiles"] = i + 1
             if X0 <= step < X0 + 4:
@@ -325,8 +329,3 @@ def tile_multiheadedattention_pa_t_kernel(tc, q, k, image_feat, W3, b3, out):
                 project((step - I0) // 4, (step - I0) % 4)
             if step in (I0 + 4, I0 + 8):
                 quantise_imf((step - I0) // 4 - 1)
-            h, n = divmod(step + 6, NQ)
-            if 0 < step + 6 < NT and n % 8 == 0:
-                prep_q(h, n // 8)
-            if 0 < step + 8 < NT and (step + 8) % NQ == 0:
-                prep_k((step + 8) // NQ)

@@ -22,8 +22,10 @@ NB = SK // P
 GRP = 4
 SCALE = 1.0 / math.sqrt(DK)
 FLOPS = 2 * SK * D * D + 2 * 2 * H * SQ * SK * DK
-EC_BUFS = 20
-X0, W0, I0, PV0 = 2, 6, 9, 19
+EC_BUFS = 28
+X0, W0, PV0 = 2, 6, 23
+EVEN0 = 48
+PROJECTIONS = [step for step in range(10, 19) if step % 8 != 1]
 LEAD = 2
 
 
@@ -110,7 +112,7 @@ def tile_multiheadedattention_pa_t_kernel(tc, q, k, image_feat, W3, b3, out):
         ic = const.tile([P, 2, D], U32, name="ic", align_bytes=64)
         isc = const.tile([P, 2, D], U8, name="isc", align_bytes=64)
 
-        def words_to_k_on_partitions(raw, grouped, pair):
+        def words_to_k_on_partitions(raw, grouped, pair, copy):
             raw32 = raw[:].bitcast(F32)
             grouped32 = grouped[:].bitcast(F32)
             px = ps_o.tile([P, 2, 2, P], F32, name="px", tag="pv")
@@ -118,7 +120,7 @@ def tile_multiheadedattention_pa_t_kernel(tc, q, k, image_feat, W3, b3, out):
                 for u in range(2):
                     c0 = (2 * pair + a) * (D // 2) + u * P
                     nc.tensor.transpose(px[:, a, u, :], raw32[:, c0 : c0 + P], ident_f[:])
-            nc.vector.tensor_copy(
+            copy(
                 out=grouped32[:, pair * 512 : (pair + 1) * 512].rearrange(
                     "p (a r u) -> p a r u", a=2, u=2
                 ),
@@ -190,7 +192,7 @@ def tile_multiheadedattention_pa_t_kernel(tc, q, k, image_feat, W3, b3, out):
         def shift(i):
             mx = mx_t[i]
             nb = stat.tile([P, 1], F32, name="nb", tag="nb")
-            nc.vector.tensor_scalar(
+            nc.gpsimd.tensor_scalar(
                 out=nb[:], in0=mx[:, 0:1], scalar1=mx[:, 1:2], scalar2=-SCALE, op0=ALU.max, op1=ALU.mult
             )
             nb_t[i] = nb
@@ -218,9 +220,10 @@ def tile_multiheadedattention_pa_t_kernel(tc, q, k, image_feat, W3, b3, out):
                 nc.tensor.transpose(et[:, m, :], words[:, m * P : (m + 1) * P], ident_f[:])
             et_t[i] = et
 
-        def regroup(i):
+        def regroup(i, engine):
             eg = work.tile([P, SK], BF16, name="eg", tag="eg", align_bytes=64)
-            nc.scalar.copy(
+            copy = nc.vector.tensor_copy if engine == "vector" else nc.scalar.copy
+            copy(
                 out=eg[:].bitcast(F32).rearrange("p (g r u) -> p g r u", g=2, u=2),
                 in_=et_t[i][:].rearrange("p (g u) r -> p g r u", g=2),
             )
@@ -253,7 +256,7 @@ def tile_multiheadedattention_pa_t_kernel(tc, q, k, image_feat, W3, b3, out):
 
         def row_sum(grp):
             rsum = sums.tile([P, GRP], F32, name="rsum", tag="rsum")
-            nc.vector.tensor_tensor(out=rsum[:], in0=rs_t[grp][:, :, 0], in1=rs_t[grp][:, :, 1], op=ALU.add)
+            nc.gpsimd.tensor_tensor(out=rsum[:], in0=rs_t[grp][:, :, 0], in1=rs_t[grp][:, :, 1], op=ALU.add)
             rsum_t[grp] = rsum
 
         def invert(grp):
@@ -287,6 +290,9 @@ def tile_multiheadedattention_pa_t_kernel(tc, q, k, image_feat, W3, b3, out):
         pooled = {"tiles": 0, "groups": 0}
         for step in range(-LEAD, NT + 7):
             ahead = step + LEAD
+            if pooled["tiles"] >= GRP * (pooled["groups"] + 1):
+                finish(pooled["groups"])
+                pooled["groups"] = pooled["groups"] + 1
             if live(ahead):
                 scores(ahead)
                 row_max(ahead)
@@ -294,9 +300,6 @@ def tile_multiheadedattention_pa_t_kernel(tc, q, k, image_feat, W3, b3, out):
                 quantise(step - 3)
             if live(ahead):
                 shift(ahead)
-            if pooled["tiles"] >= GRP * (pooled["groups"] + 1):
-                finish(pooled["groups"])
-                pooled["groups"] = pooled["groups"] + 1
             if live(step - 1) and (step - 1) % GRP == GRP - 1:
                 row_sum((step - 1) // GRP)
             if live(step - 2) and (step - 2) % GRP == GRP - 1:
@@ -305,27 +308,29 @@ def tile_multiheadedattention_pa_t_kernel(tc, q, k, image_feat, W3, b3, out):
                 exponent(step)
             if live(step - 1):
                 flip(step - 1)
-                regroup(step - 1)
+                regroup(step - 1, "vector" if step >= EVEN0 and step % 8 == 6 else "scalar")
             h, n = divmod(step + 7, NQ)
             if 0 < step + 7 < NT and n % 8 == 0:
                 prep_q(h, n // 8)
-            if 0 < step + 8 < NT and (step + 8) % NQ == 0:
-                prep_k((step + 8) // NQ, ps_o, "pv")
+            if 0 < step + 11 < NT and (step + 11) % NQ == 0:
+                prep_k((step + 11) // NQ, ps_o, "pv")
             if step >= PV0 and pooled["tiles"] == GRP * pooled["groups"] or pooled["tiles"] >= NT - GRP:
                 end = min(pooled["tiles"] - pooled["tiles"] % GRP + GRP, NT)
-                if end == NT or end <= step - 3 and step % 2 == 1:
+                if end == NT or end <= step - 3 and step % 2 == 1 and step % 8 != 1:
                     for i in range(pooled["tiles"], min(end, step - 3)):
                         pool_features(i)
                         pooled["tiles"] = i + 1
             if X0 <= step < X0 + 4:
-                words_to_k_on_partitions(x_raw, xg, step - X0)
+                words_to_k_on_partitions(x_raw, xg, step - X0, nc.scalar.copy)
             if step in (X0 + 2, X0 + 4):
                 quantise_x((step - X0) // 2 - 1)
             if W0 <= step < W0 + 2:
-                words_to_k_on_partitions(w_raw, wg, step - W0)
+                words_to_k_on_partitions(w_raw, wg, step - W0, nc.vector.tensor_copy)
             if step == W0 + 2:
                 quantise_w()
-            if I0 <= step < I0 + 8:
-                project((step - I0) // 4, (step - I0) % 4)
-            if step in (I0 + 4, I0 + 8):
-                quantise_imf((step - I0) // 4 - 1)
+            if step in PROJECTIONS:
+                piece = PROJECTIONS.index(step)
+                project(piece // 4, piece % 4)
+            for g in range(2):
+                if step == PROJECTIONS[4 * g + 3] + 1:
+                    quantise_imf(g)

@@ -25,7 +25,7 @@ FLOPS = 2 * SK * D * D + 2 * 2 * H * SQ * SK * DK
 EC_BUFS = 28
 X0, W0, PV0 = 2, 6, 23
 EVEN0 = 48
-PROJECTIONS = [step for step in range(10, 19) if step % 8 != 1]
+PROJECTIONS = [step for step in range(10, 20) if step % 8 != 1 and step != 13]
 LEAD = 2
 
 
@@ -59,15 +59,18 @@ def tile_multiheadedattention_pa_t_kernel(tc, q, k, image_feat, W3, b3, out):
         k_raw = const.tile([P, H, NB, DK], BF16, name="k_raw")
         q_raws = []
         for h in range(H):
-            nc.sync.dma_start(
-                out=k_raw[:, h, :, :].rearrange("p (g t) d -> p g (t d)", g=2),
-                in_=kf[h * SK : (h + 1) * SK, :].rearrange("(g p t) d -> p g (t d)", g=2, t=4),
-            )
+            k_dst = k_raw[:, h, :, :].rearrange("p (g t) d -> p g (t d)", g=2)
+            k_src = kf[h * SK : (h + 1) * SK, :].rearrange("(g p t) d -> p g (t d)", g=2, t=4)
+            if h == 0:
+                nc.sync.dma_start(out=k_dst[:, 0:1, :], in_=k_src[:, 0:1, :])
+            else:
+                nc.sync.dma_start(out=k_dst, in_=k_src)
             q_raw = qraw_pool.tile([P, NQ, DK], BF16, name="q_raw", tag="q_raw")
             q_src = qf[h * SQ : (h + 1) * SQ, :].rearrange("(p n) d -> p n d", n=NQ)
             if h == 0:
-                for r in range(2):
-                    nc.sync.dma_start(out=q_raw[:, 8 * r : 8 * r + 8, :], in_=q_src[:, 8 * r : 8 * r + 8, :])
+                nc.sync.dma_start(out=q_raw[:, 0:8, :], in_=q_src[:, 0:8, :])
+                nc.sync.dma_start(out=k_dst[:, 1:2, :], in_=k_src[:, 1:2, :])
+                nc.sync.dma_start(out=q_raw[:, 8:16, :], in_=q_src[:, 8:16, :])
                 nc.sync.dma_start(
                     out=x_raw[:].rearrange("p (g w) -> p g w", g=2),
                     in_=xf.rearrange("(g p t) c -> p g (t c)", g=2, t=4),
@@ -85,22 +88,22 @@ def tile_multiheadedattention_pa_t_kernel(tc, q, k, image_feat, W3, b3, out):
         kT = const.tile([P, H, SK], BF16, name="kT")
         qTs = {}
 
-        def prep_k(h, bank, tag):
-            pk = bank.tile([P, NB, P], BF16, name="pk", tag=tag)
-            for n in range(NB):
-                nc.tensor.transpose(pk[:, n, :], k_raw[:, h, n, :], ident_b[:])
-            nc.vector.tensor_copy(
-                out=kT[:, h, :].rearrange("p (a r e) -> p a r e", a=4, e=2),
-                in_=pk[:].rearrange("p (a e) r -> p a r e", e=2),
+        def prep_k(h, g, bank, tag, copy):
+            pk = bank.tile([P, 4, P], BF16, name="pk", tag=tag)
+            for t in range(4):
+                nc.tensor.transpose(pk[:, t, :], k_raw[:, h, 4 * g + t, :], ident_b[:])
+            copy(
+                out=kT[:, h, g * 512 : (g + 1) * 512].rearrange("p (u r e) -> p u r e", u=2, e=2),
+                in_=pk[:].rearrange("p (u e) r -> p u r e", e=2),
             )
 
-        def prep_q(h, r):
+        def prep_q(h, r, bank, tag, copy):
             if r == 0:
                 qTs[h] = qt_pool.tile([P, NQ, P], BF16, name="qT", tag="qT")
-            pq = ps_o.tile([P, 8, P], BF16, name="pq", tag="pv")
+            pq = bank.tile([P, 8, P], BF16, name="pq", tag=tag)
             for a in range(8):
                 nc.tensor.transpose(pq[:, a, :], q_raws[h][:, 8 * r + a, :], ident_b[:])
-            nc.vector.tensor_copy(out=qTs[h][:, 8 * r : 8 * r + 8, :], in_=pq[:])
+            copy(out=qTs[h][:, 8 * r : 8 * r + 8, :], in_=pq[:])
 
         xg = const.tile([P, SK * 4], BF16, name="xg", align_bytes=64)
         wg = const.tile([P, D * 4], BF16, name="wg", align_bytes=64)
@@ -285,8 +288,9 @@ def tile_multiheadedattention_pa_t_kernel(tc, q, k, image_feat, W3, b3, out):
             return 0 <= i < NT
 
         ctx.enter_context(tc.manual_schedule())
-        prep_k(0, ps_t, "et")
-        prep_q(0, 0)
+        prep_k(0, 0, ps_t, "et", nc.vector.tensor_copy)
+        prep_q(0, 0, ps_s, "s", nc.scalar.copy)
+        prep_k(0, 1, ps_o, "pv", nc.vector.tensor_copy)
         pooled = {"tiles": 0, "groups": 0}
         for step in range(-LEAD, NT + 7):
             ahead = step + LEAD
@@ -308,12 +312,14 @@ def tile_multiheadedattention_pa_t_kernel(tc, q, k, image_feat, W3, b3, out):
                 exponent(step)
             if live(step - 1):
                 flip(step - 1)
-                regroup(step - 1, "vector" if step >= EVEN0 and step % 8 == 6 else "scalar")
+                regroup(step - 1, "vector" if step >= EVEN0 and step % 4 == 2 else "scalar")
             h, n = divmod(step + 7, NQ)
             if 0 < step + 7 < NT and n % 8 == 0:
-                prep_q(h, n // 8)
-            if 0 < step + 11 < NT and (step + 11) % NQ == 0:
-                prep_k((step + 11) // NQ, ps_o, "pv")
+                prep_q(h, n // 8, ps_o, "pv", nc.scalar.copy if step < PV0 else nc.vector.tensor_copy)
+            for g in range(2):
+                h, n = divmod(step + 19 - 8 * g, NQ)
+                if 0 < h < H and n == 0:
+                    prep_k(h, g, ps_o, "pv", nc.scalar.copy)
             if step >= PV0 and pooled["tiles"] == GRP * pooled["groups"] or pooled["tiles"] >= NT - GRP:
                 end = min(pooled["tiles"] - pooled["tiles"] % GRP + GRP, NT)
                 if end == NT or end <= step - 3 and step % 2 == 1 and step % 8 != 1:
@@ -325,7 +331,7 @@ def tile_multiheadedattention_pa_t_kernel(tc, q, k, image_feat, W3, b3, out):
             if step in (X0 + 2, X0 + 4):
                 quantise_x((step - X0) // 2 - 1)
             if W0 <= step < W0 + 2:
-                words_to_k_on_partitions(w_raw, wg, step - W0, nc.vector.tensor_copy)
+                words_to_k_on_partitions(w_raw, wg, step - W0, nc.scalar.copy)
             if step == W0 + 2:
                 quantise_w()
             if step in PROJECTIONS:

@@ -24,7 +24,7 @@ SCALE = 1.0 / math.sqrt(DK)
 FLOPS = 2 * SK * D * D + 2 * 2 * H * SQ * SK * DK
 EC_BUFS = 28
 X0, W0, PV0 = 2, 6, 23
-EVEN0 = 48
+EVEN0 = 24
 PROJECTIONS = [step for step in range(10, 20) if step % 8 != 1 and step != 13]
 LEAD = 2
 
@@ -45,8 +45,7 @@ def tile_multiheadedattention_pa_t_kernel(tc, q, k, image_feat, W3, b3, out):
         stat = ctx.enter_context(tc.tile_pool(name="stat", bufs=4))
         sums = ctx.enter_context(tc.tile_pool(name="sums", bufs=8))
         ps_s = ctx.enter_context(tc.psum_pool(name="ps_s", bufs=6))
-        ps_t = ctx.enter_context(tc.psum_pool(name="ps_t", bufs=1))
-        ps_o = ctx.enter_context(tc.psum_pool(name="ps_o", bufs=1))
+        ps_t = ctx.enter_context(tc.psum_pool(name="ps_t", bufs=2))
 
         ident_b = const.tile([P, P], BF16, name="ident_b")
         make_identity(nc, ident_b[:])
@@ -118,7 +117,7 @@ def tile_multiheadedattention_pa_t_kernel(tc, q, k, image_feat, W3, b3, out):
         def words_to_k_on_partitions(raw, grouped, pair, copy):
             raw32 = raw[:].bitcast(F32)
             grouped32 = grouped[:].bitcast(F32)
-            px = ps_o.tile([P, 2, 2, P], F32, name="px", tag="pv")
+            px = ps_t.tile([P, 2, 2, P], F32, name="px", tag="et")
             for a in range(2):
                 for u in range(2):
                     c0 = (2 * pair + a) * (D // 2) + u * P
@@ -142,7 +141,7 @@ def tile_multiheadedattention_pa_t_kernel(tc, q, k, image_feat, W3, b3, out):
 
         def project(g, h):
             hs = slice(h * DK, (h + 1) * DK)
-            pi = ps_o.tile([P, 4, DK], F32, name="pi", tag="pv")
+            pi = ps_t.tile([P, 4, DK], F32, name="pi", tag="et")
             for t in range(4):
                 bs = slice((4 * g + t) * P, (4 * g + t + 1) * P)
                 nc.tensor.matmul_mx(
@@ -171,26 +170,22 @@ def tile_multiheadedattention_pa_t_kernel(tc, q, k, image_feat, W3, b3, out):
         s_t, nb_t, e_t, et_t, eg_t, ec_t, es_t, rs_t, pv_t = {}, {}, {}, {}, {}, {}, {}, {}, {}
         rsum_t, rcp_t, mx_t = {}, {}, {}
 
-        def scores(i):
+        def scores(i, c):
             h, n = divmod(i, NQ)
-            banks = []
-            for c in range(2):
-                s = ps_s.tile([P, 512], F32, name="s", tag="s")
-                nc.tensor.matmul(
-                    out=s[:],
-                    lhsT=qTs[h][:, n, :],
-                    rhs=kT[:, h, c * 512 : (c + 1) * 512],
-                    start=True,
-                    stop=True,
-                )
-                banks.append(s)
-            s_t[i] = banks
+            s = ps_s.tile([P, 512], F32, name="s", tag="s")
+            nc.tensor.matmul(
+                out=s[:],
+                lhsT=qTs[h][:, n, :],
+                rhs=kT[:, h, c * 512 : (c + 1) * 512],
+                start=True,
+                stop=True,
+            )
+            s_t[i, c] = s
 
-        def row_max(i):
-            mx = stat.tile([P, 2], F32, name="mx", tag="mx")
-            for c in range(2):
-                nc.vector.tensor_reduce(out=mx[:, c : c + 1], in_=s_t[i][c][:], axis=AX.X, op=ALU.max)
-            mx_t[i] = mx
+        def row_max(i, c):
+            if c == 0:
+                mx_t[i] = stat.tile([P, 2], F32, name="mx", tag="mx")
+            nc.vector.tensor_reduce(out=mx_t[i][:, c : c + 1], in_=s_t[i, c][:], axis=AX.X, op=ALU.max)
 
         def shift(i):
             mx = mx_t[i]
@@ -208,7 +203,7 @@ def tile_multiheadedattention_pa_t_kernel(tc, q, k, image_feat, W3, b3, out):
             for c in range(2):
                 nc.scalar.activation(
                     out=e[:, c * 512 : (c + 1) * 512],
-                    in_=s_t[i][c][:],
+                    in_=s_t[i, c][:],
                     func=ACTF.Exp,
                     bias=nb_t[i][:],
                     scale=SCALE,
@@ -242,7 +237,7 @@ def tile_multiheadedattention_pa_t_kernel(tc, q, k, image_feat, W3, b3, out):
         def pool_features(i):
             h = i // NQ
             if i % GRP == 0:
-                pv_t[i // GRP] = ps_o.tile([P, GRP, DK], F32, name="pv", tag="pv")
+                pv_t[i // GRP] = ps_t.tile([P, GRP, DK], F32, name="et", tag="et")
             pv = pv_t[i // GRP]
             hs = slice(h * DK, (h + 1) * DK)
             for g in range(2):
@@ -290,36 +285,45 @@ def tile_multiheadedattention_pa_t_kernel(tc, q, k, image_feat, W3, b3, out):
         ctx.enter_context(tc.manual_schedule())
         prep_k(0, 0, ps_t, "et", nc.vector.tensor_copy)
         prep_q(0, 0, ps_s, "s", nc.scalar.copy)
-        prep_k(0, 1, ps_o, "pv", nc.vector.tensor_copy)
+        prep_k(0, 1, ps_t, "et", nc.vector.tensor_copy)
         pooled = {"tiles": 0, "groups": 0}
         for step in range(-LEAD, NT + 7):
             ahead = step + LEAD
+            regrouper = "vector" if step >= EVEN0 and step % 8 == 6 else "scalar"
+            if live(ahead):
+                scores(ahead, 0)
+            if live(ahead):
+                scores(ahead, 1)
+            if live(step - 1):
+                flip(step - 1)
             if pooled["tiles"] >= GRP * (pooled["groups"] + 1):
                 finish(pooled["groups"])
                 pooled["groups"] = pooled["groups"] + 1
             if live(ahead):
-                scores(ahead)
-                row_max(ahead)
+                row_max(ahead, 0)
+            if live(step - 1) and regrouper == "vector":
+                regroup(step - 1, regrouper)
+            if live(ahead):
+                row_max(ahead, 1)
             if live(step - 3):
                 quantise(step - 3)
             if live(ahead):
                 shift(ahead)
+            if live(step):
+                exponent(step)
+            if live(step - 1) and regrouper == "scalar":
+                regroup(step - 1, regrouper)
             if live(step - 1) and (step - 1) % GRP == GRP - 1:
                 row_sum((step - 1) // GRP)
             if live(step - 2) and (step - 2) % GRP == GRP - 1:
                 invert((step - 2) // GRP)
-            if live(step):
-                exponent(step)
-            if live(step - 1):
-                flip(step - 1)
-                regroup(step - 1, "vector" if step >= EVEN0 and step % 4 == 2 else "scalar")
             h, n = divmod(step + 7, NQ)
             if 0 < step + 7 < NT and n % 8 == 0:
-                prep_q(h, n // 8, ps_o, "pv", nc.scalar.copy if step < PV0 else nc.vector.tensor_copy)
+                prep_q(h, n // 8, ps_t, "et", nc.vector.tensor_copy)
             for g in range(2):
                 h, n = divmod(step + 19 - 8 * g, NQ)
                 if 0 < h < H and n == 0:
-                    prep_k(h, g, ps_o, "pv", nc.scalar.copy)
+                    prep_k(h, g, ps_t, "et", nc.scalar.copy)
             if step >= PV0 and pooled["tiles"] == GRP * pooled["groups"] or pooled["tiles"] >= NT - GRP:
                 end = min(pooled["tiles"] - pooled["tiles"] % GRP + GRP, NT)
                 if end == NT or end <= step - 3 and step % 2 == 1 and step % 8 != 1:
@@ -327,7 +331,7 @@ def tile_multiheadedattention_pa_t_kernel(tc, q, k, image_feat, W3, b3, out):
                         pool_features(i)
                         pooled["tiles"] = i + 1
             if X0 <= step < X0 + 4:
-                words_to_k_on_partitions(x_raw, xg, step - X0, nc.scalar.copy)
+                words_to_k_on_partitions(x_raw, xg, step - X0, nc.vector.tensor_copy)
             if step in (X0 + 2, X0 + 4):
                 quantise_x((step - X0) // 2 - 1)
             if W0 <= step < W0 + 2:

@@ -20,9 +20,14 @@ NQ = SQ // P
 NT = H * NQ
 NB = SK // P
 GRP = 4
+ONES = [(i, 1) for i in range(NT - GRP, NT)]
+GROUPS = [(i, GRP) for i in range(0, NT - GRP, GRP)] + ONES
+UNITS = [(i, 2) for i in range(0, NT - GRP, 2)] + ONES
+GROUP_OF = {i: g for g, (first, count) in enumerate(GROUPS) for i in range(first, first + count)}
+UNIT_OF = {i: v for v, (first, count) in enumerate(UNITS) for i in range(first, first + count)}
 SCALE = 1.0 / math.sqrt(DK)
 FLOPS = 2 * SK * D * D + 2 * 2 * H * SQ * SK * DK
-EC_BUFS = 28
+EC_BUFS = 14
 X0, W0, PV0 = 2, 6, 23
 EVEN0 = 24
 PROJECTIONS = [step for step in range(10, 20) if step % 8 != 1 and step != 13]
@@ -67,9 +72,9 @@ def tile_multiheadedattention_pa_t_kernel(tc, q, k, image_feat, W3, b3, out):
             q_raw = qraw_pool.tile([P, NQ, DK], BF16, name="q_raw", tag="q_raw")
             q_src = qf[h * SQ : (h + 1) * SQ, :].rearrange("(p n) d -> p n d", n=NQ)
             if h == 0:
-                nc.sync.dma_start(out=q_raw[:, 0:8, :], in_=q_src[:, 0:8, :])
+                nc.sync.dma_start(out=q_raw[:, 0:4, :], in_=q_src[:, 0:4, :])
                 nc.sync.dma_start(out=k_dst[:, 1:2, :], in_=k_src[:, 1:2, :])
-                nc.sync.dma_start(out=q_raw[:, 8:16, :], in_=q_src[:, 8:16, :])
+                nc.sync.dma_start(out=q_raw[:, 4:16, :], in_=q_src[:, 4:16, :])
                 nc.sync.dma_start(
                     out=x_raw[:].rearrange("p (g w) -> p g w", g=2),
                     in_=xf.rearrange("(g p t) c -> p g (t c)", g=2, t=4),
@@ -96,13 +101,13 @@ def tile_multiheadedattention_pa_t_kernel(tc, q, k, image_feat, W3, b3, out):
                 in_=pk[:].rearrange("p (u e) r -> p u r e", e=2),
             )
 
-        def prep_q(h, r, bank, tag, copy):
-            if r == 0:
+        def prep_q(h, first, count, bank, tag, copy):
+            if first == 0:
                 qTs[h] = qt_pool.tile([P, NQ, P], BF16, name="qT", tag="qT")
-            pq = bank.tile([P, 8, P], BF16, name="pq", tag=tag)
-            for a in range(8):
-                nc.tensor.transpose(pq[:, a, :], q_raws[h][:, 8 * r + a, :], ident_b[:])
-            copy(out=qTs[h][:, 8 * r : 8 * r + 8, :], in_=pq[:])
+            pq = bank.tile([P, count, P], BF16, name="pq", tag=tag)
+            for a in range(count):
+                nc.tensor.transpose(pq[:, a, :], q_raws[h][:, first + a, :], ident_b[:])
+            copy(out=qTs[h][:, first : first + count, :], in_=pq[:])
 
         xg = const.tile([P, SK * 4], BF16, name="xg", align_bytes=64)
         wg = const.tile([P, D * 4], BF16, name="wg", align_bytes=64)
@@ -196,9 +201,10 @@ def tile_multiheadedattention_pa_t_kernel(tc, q, k, image_feat, W3, b3, out):
             nb_t[i] = nb
 
         def exponent(i):
-            if i % GRP == 0:
-                rs_t[i // GRP] = sums.tile([P, GRP, 2], F32, name="rs", tag="rs")
-            rs = rs_t[i // GRP]
+            first, count = GROUPS[GROUP_OF[i]]
+            if i == first:
+                rs_t[GROUP_OF[i]] = sums.tile([P, count, 2], F32, name="rs", tag="rs")
+            rs = rs_t[GROUP_OF[i]]
             e = work.tile([P, SK], BF16, name="e", tag="e")
             for c in range(2):
                 nc.scalar.activation(
@@ -207,7 +213,7 @@ def tile_multiheadedattention_pa_t_kernel(tc, q, k, image_feat, W3, b3, out):
                     func=ACTF.Exp,
                     bias=nb_t[i][:],
                     scale=SCALE,
-                    accum_out=rs[:, i % GRP, c : c + 1],
+                    accum_out=rs[:, i - first, c : c + 1],
                 )
             e_t[i] = e
 
@@ -219,33 +225,44 @@ def tile_multiheadedattention_pa_t_kernel(tc, q, k, image_feat, W3, b3, out):
             et_t[i] = et
 
         def regroup(i, engine):
-            eg = work.tile([P, SK], BF16, name="eg", tag="eg", align_bytes=64)
+            unit = UNIT_OF[i]
+            first, count = UNITS[unit]
+            if i == first:
+                eg_t[unit] = work.tile([P, count, SK], BF16, name="eg", tag="eg", align_bytes=64)
             copy = nc.vector.tensor_copy if engine == "vector" else nc.scalar.copy
             copy(
-                out=eg[:].bitcast(F32).rearrange("p (g r u) -> p g r u", g=2, u=2),
+                out=eg_t[unit][:, i - first, :].bitcast(F32).rearrange("p (g r u) -> p g r u", g=2, u=2),
                 in_=et_t[i][:].rearrange("p (g u) r -> p g r u", g=2),
             )
-            eg_t[i] = eg
 
-        def quantise(i):
-            ec = codes.tile([P, 2 * P], U32, name="ec", tag="ec", align_bytes=64)
-            es = codes.tile([P, 2 * P], U8, name="es", tag="es", align_bytes=64)
-            nc.vector.quantize_mx(out=ec[:].bitcast(FP8X4), scales=es[:], in_=eg_t[i][:])
-            ec_t[i] = ec
-            es_t[i] = es
+        def quantise(unit):
+            words = UNITS[unit][1] * 2 * P
+            ec = codes.tile([P, words], U32, name="ec", tag="ec", align_bytes=64)
+            es = codes.tile([P, words], U8, name="es", tag="es", align_bytes=64)
+            nc.vector.quantize_mx(
+                out=ec[:].bitcast(FP8X4), scales=es[:], in_=eg_t[unit][:].rearrange("p a k -> p (a k)")
+            )
+            ec_t[unit] = ec
+            es_t[unit] = es
 
         def pool_features(i):
             h = i // NQ
-            if i % GRP == 0:
-                pv_t[i // GRP] = ps_t.tile([P, GRP, DK], F32, name="et", tag="et")
-            pv = pv_t[i // GRP]
+            grp = GROUP_OF[i]
+            first, count = GROUPS[grp]
+            if i == first and count == GRP:
+                pv_t[grp] = ps_t.tile([P, GRP, DK], F32, name="pv", tag="et")
+            elif i == first:
+                pv_t[grp] = ps_s.tile([P, count, DK], F32, name="pv", tag="s")
+            pv = pv_t[grp]
             hs = slice(h * DK, (h + 1) * DK)
+            unit = UNIT_OF[i]
             for g in range(2):
-                gs = slice(g * P, (g + 1) * P)
+                block = 2 * (i - UNITS[unit][0]) + g
+                bs = slice(block * P, (block + 1) * P)
                 nc.tensor.matmul_mx(
-                    out=pv[:, i % GRP, :],
-                    lhsT=ec_t[i][:, gs].bitcast(FP8X4),
-                    lhsT_scale=es_t[i][:, gs],
+                    out=pv[:, i - first, :],
+                    lhsT=ec_t[unit][:, bs].bitcast(FP8X4),
+                    lhsT_scale=es_t[unit][:, bs],
                     rhs=ic[:, g, hs].bitcast(FP8X4),
                     rhs_scale=isc[:, g, hs],
                     start=(g == 0),
@@ -253,40 +270,41 @@ def tile_multiheadedattention_pa_t_kernel(tc, q, k, image_feat, W3, b3, out):
                 )
 
         def row_sum(grp):
-            rsum = sums.tile([P, GRP], F32, name="rsum", tag="rsum")
+            rsum = sums.tile([P, GROUPS[grp][1]], F32, name="rsum", tag="rsum")
             nc.gpsimd.tensor_tensor(out=rsum[:], in0=rs_t[grp][:, :, 0], in1=rs_t[grp][:, :, 1], op=ALU.add)
             rsum_t[grp] = rsum
 
         def invert(grp):
-            rcp = sums.tile([P, GRP], F32, name="rcp", tag="rcp")
+            rcp = sums.tile([P, GROUPS[grp][1]], F32, name="rcp", tag="rcp")
             nc.vector.reciprocal(out=rcp[:], in_=rsum_t[grp][:])
             rcp_t[grp] = rcp
 
         def finish(grp):
-            h, m = divmod(grp, NQ // GRP)
-            rcp = rcp_t[grp]
-            o_sb = work.tile([P, GRP, DK], F32, name="o_sb", tag="o_sb")
+            first, count = GROUPS[grp]
+            h, n = divmod(first, NQ)
+            o_sb = work.tile([P, count, DK], F32, name="o_sb", tag="o_sb")
             nc.vector.tensor_tensor(
                 out=o_sb[:],
                 in0=pv_t[grp][:],
-                in1=rcp[:].unsqueeze(2).to_broadcast([P, GRP, DK]),
+                in1=rcp_t[grp][:].unsqueeze(2).to_broadcast([P, count, DK]),
                 op=ALU.mult,
             )
             nc.sync.dma_start(
-                out=of[h * SQ : (h + 1) * SQ, :].rearrange("(p n) d -> p n d", n=NQ)[
-                    :, m * GRP : (m + 1) * GRP, :
-                ],
+                out=of[h * SQ : (h + 1) * SQ, :].rearrange("(p n) d -> p n d", n=NQ)[:, n : n + count, :],
                 in_=o_sb[:],
             )
 
         def live(i):
             return 0 <= i < NT
 
+        def last_of_group(i):
+            return i == NT - 1 or GROUP_OF[i + 1] != GROUP_OF[i]
+
         ctx.enter_context(tc.manual_schedule())
         prep_k(0, 0, ps_t, "et", nc.vector.tensor_copy)
-        prep_q(0, 0, ps_s, "s", nc.scalar.copy)
+        prep_q(0, 0, 4, ps_s, "s", nc.scalar.copy)
         prep_k(0, 1, ps_t, "et", nc.vector.tensor_copy)
-        pooled = {"tiles": 0, "groups": 0}
+        quantised = pooled = emptied = 0
         for step in range(-LEAD, NT + 7):
             ahead = step + LEAD
             regrouper = "vector" if step >= EVEN0 and step % 8 == 6 else "scalar"
@@ -296,40 +314,43 @@ def tile_multiheadedattention_pa_t_kernel(tc, q, k, image_feat, W3, b3, out):
                 scores(ahead, 1)
             if live(step - 1):
                 flip(step - 1)
-            if pooled["tiles"] >= GRP * (pooled["groups"] + 1):
-                finish(pooled["groups"])
-                pooled["groups"] = pooled["groups"] + 1
+            if emptied < pooled:
+                finish(emptied)
+                emptied += 1
             if live(ahead):
                 row_max(ahead, 0)
             if live(step - 1) and regrouper == "vector":
                 regroup(step - 1, regrouper)
             if live(ahead):
                 row_max(ahead, 1)
-            if live(step - 3):
-                quantise(step - 3)
+            if quantised < len(UNITS) and sum(UNITS[quantised]) <= step - 1:
+                quantise(quantised)
+                quantised += 1
             if live(ahead):
                 shift(ahead)
             if live(step):
                 exponent(step)
             if live(step - 1) and regrouper == "scalar":
                 regroup(step - 1, regrouper)
-            if live(step - 1) and (step - 1) % GRP == GRP - 1:
-                row_sum((step - 1) // GRP)
-            if live(step - 2) and (step - 2) % GRP == GRP - 1:
-                invert((step - 2) // GRP)
+            if live(step - 1) and last_of_group(step - 1):
+                row_sum(GROUP_OF[step - 1])
+            if live(step - 2) and last_of_group(step - 2):
+                invert(GROUP_OF[step - 2])
+            if step == -1:
+                prep_q(0, 4, 4, ps_t, "et", nc.scalar.copy)
             h, n = divmod(step + 7, NQ)
             if 0 < step + 7 < NT and n % 8 == 0:
-                prep_q(h, n // 8, ps_t, "et", nc.vector.tensor_copy)
+                prep_q(h, n, 8, ps_t, "et", nc.vector.tensor_copy)
             for g in range(2):
                 h, n = divmod(step + 19 - 8 * g, NQ)
                 if 0 < h < H and n == 0:
                     prep_k(h, g, ps_t, "et", nc.scalar.copy)
-            if step >= PV0 and pooled["tiles"] == GRP * pooled["groups"] or pooled["tiles"] >= NT - GRP:
-                end = min(pooled["tiles"] - pooled["tiles"] % GRP + GRP, NT)
-                if end == NT or end <= step - 3 and step % 2 == 1 and step % 8 != 1:
-                    for i in range(pooled["tiles"], min(end, step - 3)):
+            if step >= PV0 and pooled < len(GROUPS) and emptied == pooled:
+                first, count = GROUPS[pooled]
+                if first + count <= step - 2 and (first >= NT - 2 * GRP or step % 2 == 1 and step % 8 != 1):
+                    for i in range(first, first + count):
                         pool_features(i)
-                        pooled["tiles"] = i + 1
+                    pooled += 1
             if X0 <= step < X0 + 4:
                 words_to_k_on_partitions(x_raw, xg, step - X0, nc.vector.tensor_copy)
             if step in (X0 + 2, X0 + 4):

@@ -31,6 +31,7 @@ EC_BUFS = 14
 X0, W0, PV0 = 2, 6, 23
 EVEN0 = 24
 PROJECTIONS = [step for step in range(10, 20) if step % 8 != 1 and step != 13]
+WARM = 12
 LEAD = 2
 
 
@@ -57,6 +58,10 @@ def tile_multiheadedattention_pa_t_kernel(tc, q, k, image_feat, W3, b3, out):
         ident_f = const.tile([P, P], F32, name="ident_f")
         make_identity(nc, ident_f[:])
 
+        warm = ps_s.tile([P, P], F32, name="warm", tag="s")
+        for n in range(WARM):
+            nc.tensor.matmul(out=warm[:], lhsT=ident_b[:], rhs=ident_b[:], start=True, stop=True)
+
         x_raw = const.tile([P, NB * D], BF16, name="x_raw")
         w_raw = const.tile([P, H * D], BF16, name="w_raw")
         b3bc = const.tile([P, D], BF16, name="b3bc")
@@ -72,9 +77,9 @@ def tile_multiheadedattention_pa_t_kernel(tc, q, k, image_feat, W3, b3, out):
             q_raw = qraw_pool.tile([P, NQ, DK], BF16, name="q_raw", tag="q_raw")
             q_src = qf[h * SQ : (h + 1) * SQ, :].rearrange("(p n) d -> p n d", n=NQ)
             if h == 0:
-                nc.sync.dma_start(out=q_raw[:, 0:4, :], in_=q_src[:, 0:4, :])
+                nc.sync.dma_start(out=q_raw[:, 0:2, :], in_=q_src[:, 0:2, :])
                 nc.sync.dma_start(out=k_dst[:, 1:2, :], in_=k_src[:, 1:2, :])
-                nc.sync.dma_start(out=q_raw[:, 4:16, :], in_=q_src[:, 4:16, :])
+                nc.sync.dma_start(out=q_raw[:, 2:16, :], in_=q_src[:, 2:16, :])
                 nc.sync.dma_start(
                     out=x_raw[:].rearrange("p (g w) -> p g w", g=2),
                     in_=xf.rearrange("(g p t) c -> p g (t c)", g=2, t=4),
@@ -302,12 +307,12 @@ def tile_multiheadedattention_pa_t_kernel(tc, q, k, image_feat, W3, b3, out):
 
         ctx.enter_context(tc.manual_schedule())
         prep_k(0, 0, ps_t, "et", nc.vector.tensor_copy)
-        prep_q(0, 0, 4, ps_s, "s", nc.scalar.copy)
+        prep_q(0, 0, 2, ps_s, "s", nc.scalar.copy)
         prep_k(0, 1, ps_t, "et", nc.vector.tensor_copy)
         quantised = pooled = emptied = 0
         for step in range(-LEAD, NT + 7):
             ahead = step + LEAD
-            regrouper = "vector" if step >= EVEN0 and step % 8 == 6 else "scalar"
+            regrouper = "vector" if step >= EVEN0 and step % 12 == 6 else "scalar"
             if live(ahead):
                 scores(ahead, 0)
             if live(ahead):
@@ -337,7 +342,7 @@ def tile_multiheadedattention_pa_t_kernel(tc, q, k, image_feat, W3, b3, out):
             if live(step - 2) and last_of_group(step - 2):
                 invert(GROUP_OF[step - 2])
             if step == -1:
-                prep_q(0, 4, 4, ps_t, "et", nc.scalar.copy)
+                prep_q(0, 2, 6, ps_t, "et", nc.scalar.copy)
             h, n = divmod(step + 7, NQ)
             if 0 < step + 7 < NT and n % 8 == 0:
                 prep_q(h, n, 8, ps_t, "et", nc.vector.tensor_copy)

@@ -24,6 +24,8 @@ ONES = [(i, 1) for i in range(NT - GRP, NT)]
 GROUPS = [(i, GRP) for i in range(0, NT - GRP, GRP)] + ONES
 UNITS = [(i, 2) for i in range(0, NT - GRP, 2)] + ONES
 GROUP_OF = {i: g for g, (first, count) in enumerate(GROUPS) for i in range(first, first + count)}
+BATCHES = [(g, 2) for g in range(0, NT // GRP - 2, 2)] + [(g, 1) for g in range(NT // GRP - 2, len(GROUPS))]
+BATCH_OF = {g: b for b, (first, count) in enumerate(BATCHES) for g in range(first, first + count)}
 UNIT_OF = {i: v for v, (first, count) in enumerate(UNITS) for i in range(first, first + count)}
 SCALE = 1.0 / math.sqrt(DK)
 FLOPS = 2 * SK * D * D + 2 * 2 * H * SQ * SK * DK
@@ -31,7 +33,7 @@ EC_BUFS = 14
 X0, W0, PV0 = 2, 6, 23
 EVEN0 = 24
 PROJECTIONS = [step for step in range(10, 20) if step % 8 != 1 and step != 13]
-WARM = 12
+WARM = 9
 LEAD = 2
 
 
@@ -70,20 +72,21 @@ def tile_multiheadedattention_pa_t_kernel(tc, q, k, image_feat, W3, b3, out):
         for h in range(H):
             k_dst = k_raw[:, h, :, :].rearrange("p (g t) d -> p g (t d)", g=2)
             k_src = kf[h * SK : (h + 1) * SK, :].rearrange("(g p t) d -> p g (t d)", g=2, t=4)
-            if h == 0:
-                nc.sync.dma_start(out=k_dst[:, 0:1, :], in_=k_src[:, 0:1, :])
-            else:
+            if h > 0:
                 nc.sync.dma_start(out=k_dst, in_=k_src)
             q_raw = qraw_pool.tile([P, NQ, DK], BF16, name="q_raw", tag="q_raw")
             q_src = qf[h * SQ : (h + 1) * SQ, :].rearrange("(p n) d -> p n d", n=NQ)
             if h == 0:
+                x_dst = x_raw[:].rearrange("p (g a w) -> p g a w", g=2, a=2)
+                x_src = xf.rearrange("(g p a t) c -> p g a (t c)", g=2, a=2, t=2)
+                nc.sync.dma_start(out=k_dst[:, 0:1, :], in_=k_src[:, 0:1, :])
                 nc.sync.dma_start(out=q_raw[:, 0:2, :], in_=q_src[:, 0:2, :])
+                nc.sync.dma_start(out=x_dst[:, 0, 0, :], in_=x_src[:, 0, 0, :])
                 nc.sync.dma_start(out=k_dst[:, 1:2, :], in_=k_src[:, 1:2, :])
-                nc.sync.dma_start(out=q_raw[:, 2:16, :], in_=q_src[:, 2:16, :])
-                nc.sync.dma_start(
-                    out=x_raw[:].rearrange("p (g w) -> p g w", g=2),
-                    in_=xf.rearrange("(g p t) c -> p g (t c)", g=2, t=4),
-                )
+                nc.sync.dma_start(out=x_dst[:, 0, 1, :], in_=x_src[:, 0, 1, :])
+                nc.sync.dma_start(out=q_raw[:, 2:8, :], in_=q_src[:, 2:8, :])
+                nc.sync.dma_start(out=x_dst[:, 1, :, :], in_=x_src[:, 1, :, :])
+                nc.sync.dma_start(out=q_raw[:, 8:16, :], in_=q_src[:, 8:16, :])
                 nc.sync.dma_start(
                     out=w_raw[:].rearrange("p (n c) -> p n c", n=H),
                     in_=W3.rearrange("(n p) c -> p n c", p=P),
@@ -124,10 +127,10 @@ def tile_multiheadedattention_pa_t_kernel(tc, q, k, image_feat, W3, b3, out):
         ic = const.tile([P, 2, D], U32, name="ic", align_bytes=64)
         isc = const.tile([P, 2, D], U8, name="isc", align_bytes=64)
 
-        def words_to_k_on_partitions(raw, grouped, pair, copy):
+        def words_to_k_on_partitions(raw, grouped, pair, bank, tag, copy):
             raw32 = raw[:].bitcast(F32)
             grouped32 = grouped[:].bitcast(F32)
-            px = ps_t.tile([P, 2, 2, P], F32, name="px", tag="et")
+            px = bank.tile([P, 2, 2, P], F32, name="px", tag=tag)
             for a in range(2):
                 for u in range(2):
                     c0 = (2 * pair + a) * (D // 2) + u * P
@@ -275,14 +278,20 @@ def tile_multiheadedattention_pa_t_kernel(tc, q, k, image_feat, W3, b3, out):
                 )
 
         def row_sum(grp):
-            rsum = sums.tile([P, GROUPS[grp][1]], F32, name="rsum", tag="rsum")
-            nc.gpsimd.tensor_tensor(out=rsum[:], in0=rs_t[grp][:, :, 0], in1=rs_t[grp][:, :, 1], op=ALU.add)
-            rsum_t[grp] = rsum
+            count = GROUPS[grp][1]
+            batch = BATCH_OF[grp]
+            first, groups = BATCHES[batch]
+            if grp == first:
+                rsum_t[batch] = sums.tile([P, groups, count], F32, name="rsum", tag="rsum")
+            nc.gpsimd.tensor_tensor(
+                out=rsum_t[batch][:, grp - first, :], in0=rs_t[grp][:, :, 0], in1=rs_t[grp][:, :, 1], op=ALU.add
+            )
 
-        def invert(grp):
-            rcp = sums.tile([P, GROUPS[grp][1]], F32, name="rcp", tag="rcp")
-            nc.vector.reciprocal(out=rcp[:], in_=rsum_t[grp][:])
-            rcp_t[grp] = rcp
+        def invert(batch):
+            first, groups = BATCHES[batch]
+            rcp = sums.tile([P, groups, GROUPS[first][1]], F32, name="rcp", tag="rcp")
+            nc.vector.reciprocal(out=rcp[:], in_=rsum_t[batch][:])
+            rcp_t[batch] = rcp
 
         def finish(grp):
             first, count = GROUPS[grp]
@@ -291,7 +300,7 @@ def tile_multiheadedattention_pa_t_kernel(tc, q, k, image_feat, W3, b3, out):
             nc.vector.tensor_tensor(
                 out=o_sb[:],
                 in0=pv_t[grp][:],
-                in1=rcp_t[grp][:].unsqueeze(2).to_broadcast([P, count, DK]),
+                in1=rcp_t[BATCH_OF[grp]][:, grp - BATCHES[BATCH_OF[grp]][0], :].unsqueeze(2).to_broadcast([P, count, DK]),
                 op=ALU.mult,
             )
             nc.sync.dma_start(
@@ -305,18 +314,26 @@ def tile_multiheadedattention_pa_t_kernel(tc, q, k, image_feat, W3, b3, out):
         def last_of_group(i):
             return i == NT - 1 or GROUP_OF[i + 1] != GROUP_OF[i]
 
+        def last_of_batch(i):
+            return last_of_group(i) and sum(BATCHES[BATCH_OF[GROUP_OF[i]]]) == GROUP_OF[i] + 1
+
         ctx.enter_context(tc.manual_schedule())
         prep_k(0, 0, ps_t, "et", nc.vector.tensor_copy)
         prep_q(0, 0, 2, ps_s, "s", nc.scalar.copy)
+        words_to_k_on_partitions(x_raw, xg, 0, ps_t, "et", nc.scalar.copy)
         prep_k(0, 1, ps_t, "et", nc.vector.tensor_copy)
         quantised = pooled = emptied = 0
         for step in range(-LEAD, NT + 7):
             ahead = step + LEAD
-            regrouper = "vector" if step >= EVEN0 and step % 12 == 6 else "scalar"
+            regrouper = "vector" if step >= EVEN0 and step % 9 == 4 or step > NT - 2 else "scalar"
             if live(ahead):
                 scores(ahead, 0)
+            if step == -LEAD:
+                words_to_k_on_partitions(x_raw, xg, 1, ps_s, "s", nc.scalar.copy)
             if live(ahead):
                 scores(ahead, 1)
+            if step == -LEAD:
+                prep_q(0, 2, 6, ps_t, "et", nc.scalar.copy)
             if live(step - 1):
                 flip(step - 1)
             if emptied < pooled:
@@ -324,13 +341,13 @@ def tile_multiheadedattention_pa_t_kernel(tc, q, k, image_feat, W3, b3, out):
                 emptied += 1
             if live(ahead):
                 row_max(ahead, 0)
+            if quantised < len(UNITS) and sum(UNITS[quantised]) <= step - 1:
+                quantise(quantised)
+                quantised += 1
             if live(step - 1) and regrouper == "vector":
                 regroup(step - 1, regrouper)
             if live(ahead):
                 row_max(ahead, 1)
-            if quantised < len(UNITS) and sum(UNITS[quantised]) <= step - 1:
-                quantise(quantised)
-                quantised += 1
             if live(ahead):
                 shift(ahead)
             if live(step):
@@ -339,10 +356,8 @@ def tile_multiheadedattention_pa_t_kernel(tc, q, k, image_feat, W3, b3, out):
                 regroup(step - 1, regrouper)
             if live(step - 1) and last_of_group(step - 1):
                 row_sum(GROUP_OF[step - 1])
-            if live(step - 2) and last_of_group(step - 2):
-                invert(GROUP_OF[step - 2])
-            if step == -1:
-                prep_q(0, 2, 6, ps_t, "et", nc.scalar.copy)
+            if live(step - 2) and last_of_batch(step - 2):
+                invert(BATCH_OF[GROUP_OF[step - 2]])
             h, n = divmod(step + 7, NQ)
             if 0 < step + 7 < NT and n % 8 == 0:
                 prep_q(h, n, 8, ps_t, "et", nc.vector.tensor_copy)
@@ -352,16 +367,17 @@ def tile_multiheadedattention_pa_t_kernel(tc, q, k, image_feat, W3, b3, out):
                     prep_k(h, g, ps_t, "et", nc.scalar.copy)
             if step >= PV0 and pooled < len(GROUPS) and emptied == pooled:
                 first, count = GROUPS[pooled]
-                if first + count <= step - 2 and (first >= NT - 2 * GRP or step % 2 == 1 and step % 8 != 1):
+                inverted = sum(GROUPS[sum(BATCHES[BATCH_OF[pooled]]) - 1])
+                if inverted <= step - 2 and (first >= NT - 3 * GRP or step % 4 == 3 or first + 3 * GRP <= step and step % 8 == 5):
                     for i in range(first, first + count):
                         pool_features(i)
                     pooled += 1
-            if X0 <= step < X0 + 4:
-                words_to_k_on_partitions(x_raw, xg, step - X0, nc.vector.tensor_copy)
+            if step in (X0 + 1, X0 + 3):
+                words_to_k_on_partitions(x_raw, xg, 2 + (step - X0) // 2, ps_t, "et", nc.vector.tensor_copy)
             if step in (X0 + 2, X0 + 4):
                 quantise_x((step - X0) // 2 - 1)
             if W0 <= step < W0 + 2:
-                words_to_k_on_partitions(w_raw, wg, step - W0, nc.scalar.copy)
+                words_to_k_on_partitions(w_raw, wg, step - W0, ps_t, "et", nc.scalar.copy)
             if step == W0 + 2:
                 quantise_w()
             if step in PROJECTIONS:

@@ -34,6 +34,7 @@ X0, W0, PV0 = 2, 6, 23
 EVEN0 = 24
 PROJECTIONS = [step for step in range(10, 20) if step % 8 != 1 and step != 13]
 WARM = 9
+TAIL = NT - 3
 LEAD = 2
 
 
@@ -81,10 +82,10 @@ def tile_multiheadedattention_pa_t_kernel(tc, q, k, image_feat, W3, b3, out):
                 x_src = xf.rearrange("(g p a t) c -> p g a (t c)", g=2, a=2, t=2)
                 nc.sync.dma_start(out=k_dst[:, 0:1, :], in_=k_src[:, 0:1, :])
                 nc.sync.dma_start(out=q_raw[:, 0:2, :], in_=q_src[:, 0:2, :])
-                nc.sync.dma_start(out=x_dst[:, 0, 0, :], in_=x_src[:, 0, 0, :])
                 nc.sync.dma_start(out=k_dst[:, 1:2, :], in_=k_src[:, 1:2, :])
-                nc.sync.dma_start(out=x_dst[:, 0, 1, :], in_=x_src[:, 0, 1, :])
+                nc.sync.dma_start(out=x_dst[:, 0, 0, :], in_=x_src[:, 0, 0, :])
                 nc.sync.dma_start(out=q_raw[:, 2:8, :], in_=q_src[:, 2:8, :])
+                nc.sync.dma_start(out=x_dst[:, 0, 1, :], in_=x_src[:, 0, 1, :])
                 nc.sync.dma_start(out=x_dst[:, 1, :, :], in_=x_src[:, 1, :, :])
                 nc.sync.dma_start(out=q_raw[:, 8:16, :], in_=q_src[:, 8:16, :])
                 nc.sync.dma_start(
@@ -227,10 +228,19 @@ def tile_multiheadedattention_pa_t_kernel(tc, q, k, image_feat, W3, b3, out):
 
         def flip(i):
             words = e_t[i][:].bitcast(F32)
-            et = ps_t.tile([P, 4, P], F32, name="et", tag="et")
+            bank, tag = (ps_t, "et") if i < TAIL else (ps_s, "s")
+            et = bank.tile([P, 4, P], F32, name="et", tag=tag)
             for m in range(4):
                 nc.tensor.transpose(et[:, m, :], words[:, m * P : (m + 1) * P], ident_f[:])
             et_t[i] = et
+
+        def flip_half(i, g):
+            words = e_t[i][:].bitcast(F32)
+            et = ps_s.tile([P, 2, P], F32, name="et", tag="s")
+            for u in range(2):
+                m = 2 * g + u
+                nc.tensor.transpose(et[:, u, :], words[:, m * P : (m + 1) * P], ident_f[:])
+            et_t[i, g] = et
 
         def regroup(i, engine):
             unit = UNIT_OF[i]
@@ -241,6 +251,27 @@ def tile_multiheadedattention_pa_t_kernel(tc, q, k, image_feat, W3, b3, out):
             copy(
                 out=eg_t[unit][:, i - first, :].bitcast(F32).rearrange("p (g r u) -> p g r u", g=2, u=2),
                 in_=et_t[i][:].rearrange("p (g u) r -> p g r u", g=2),
+            )
+
+        def regroup_half(i, g, engine):
+            unit = UNIT_OF[i]
+            if g == 0:
+                eg_t[unit] = work.tile([P, 1, SK], BF16, name="eg", tag="eg", align_bytes=64)
+            copy = nc.vector.tensor_copy if engine == "vector" else nc.scalar.copy
+            copy(
+                out=eg_t[unit][:, 0, g * 512 : (g + 1) * 512].bitcast(F32).rearrange("p (r u) -> p r u", u=2),
+                in_=et_t[i, g][:].rearrange("p u r -> p r u"),
+            )
+
+        def quantise_half(unit, g):
+            if g == 0:
+                ec_t[unit] = codes.tile([P, 2 * P], U32, name="ec", tag="ec", align_bytes=64)
+                es_t[unit] = codes.tile([P, 2 * P], U8, name="es", tag="es", align_bytes=64)
+            bs = slice(g * P, (g + 1) * P)
+            nc.vector.quantize_mx(
+                out=ec_t[unit][:, bs].bitcast(FP8X4),
+                scales=es_t[unit][:, bs],
+                in_=eg_t[unit][:, 0, g * 512 : (g + 1) * 512],
             )
 
         def quantise(unit):
@@ -320,39 +351,44 @@ def tile_multiheadedattention_pa_t_kernel(tc, q, k, image_feat, W3, b3, out):
         ctx.enter_context(tc.manual_schedule())
         prep_k(0, 0, ps_t, "et", nc.vector.tensor_copy)
         prep_q(0, 0, 2, ps_s, "s", nc.scalar.copy)
-        words_to_k_on_partitions(x_raw, xg, 0, ps_t, "et", nc.scalar.copy)
         prep_k(0, 1, ps_t, "et", nc.vector.tensor_copy)
         quantised = pooled = emptied = 0
-        for step in range(-LEAD, NT + 7):
+        for step in range(-LEAD, NT - 1):
             ahead = step + LEAD
-            regrouper = "vector" if step >= EVEN0 and step % 9 == 4 or step > NT - 2 else "scalar"
+            regrouper = "vector" if step >= EVEN0 and step % 12 == 6 else "scalar"
             if live(ahead):
                 scores(ahead, 0)
-            if step == -LEAD:
-                words_to_k_on_partitions(x_raw, xg, 1, ps_s, "s", nc.scalar.copy)
             if live(ahead):
                 scores(ahead, 1)
             if step == -LEAD:
+                words_to_k_on_partitions(x_raw, xg, 0, ps_t, "et", nc.scalar.copy)
+            if step == 1 - LEAD:
                 prep_q(0, 2, 6, ps_t, "et", nc.scalar.copy)
+                words_to_k_on_partitions(x_raw, xg, 1, ps_t, "et", nc.scalar.copy)
             if live(step - 1):
                 flip(step - 1)
+            late = ahead >= NT - 1
+            if late and live(ahead):
+                row_max(ahead, 0)
+            if late and live(ahead):
+                row_max(ahead, 1)
             if emptied < pooled:
                 finish(emptied)
                 emptied += 1
-            if live(ahead):
+            if not late and live(ahead):
                 row_max(ahead, 0)
             if quantised < len(UNITS) and sum(UNITS[quantised]) <= step - 1:
                 quantise(quantised)
                 quantised += 1
-            if live(step - 1) and regrouper == "vector":
+            if 0 <= step - 1 < TAIL and regrouper == "vector":
                 regroup(step - 1, regrouper)
-            if live(ahead):
+            if not late and live(ahead):
                 row_max(ahead, 1)
             if live(ahead):
                 shift(ahead)
             if live(step):
                 exponent(step)
-            if live(step - 1) and regrouper == "scalar":
+            if 0 <= step - 1 < TAIL and regrouper == "scalar":
                 regroup(step - 1, regrouper)
             if live(step - 1) and last_of_group(step - 1):
                 row_sum(GROUP_OF[step - 1])
@@ -368,7 +404,7 @@ def tile_multiheadedattention_pa_t_kernel(tc, q, k, image_feat, W3, b3, out):
             if step >= PV0 and pooled < len(GROUPS) and emptied == pooled:
                 first, count = GROUPS[pooled]
                 inverted = sum(GROUPS[sum(BATCHES[BATCH_OF[pooled]]) - 1])
-                if inverted <= step - 2 and (first >= NT - 3 * GRP or step % 4 == 3 or first + 3 * GRP <= step and step % 8 == 5):
+                if inverted <= step - 2 and (first >= NT - 4 * GRP or step % 4 == 3 or first + 3 * GRP <= step and step % 8 == 5):
                     for i in range(first, first + count):
                         pool_features(i)
                     pooled += 1
@@ -386,3 +422,37 @@ def tile_multiheadedattention_pa_t_kernel(tc, q, k, image_feat, W3, b3, out):
             for g in range(2):
                 if step == PROJECTIONS[4 * g + 3] + 1:
                     quantise_imf(g)
+
+        def pool_group(grp):
+            first, count = GROUPS[grp]
+            for i in range(first, first + count):
+                pool_features(i)
+
+        last = NT - 1
+        groups = len(GROUPS)
+        exponent(last)
+        flip(last - 1)
+        finish(groups - 5)
+        regroup(last - 2, "vector")
+        row_sum(groups - 2)
+        row_sum(groups - 1)
+        invert(BATCH_OF[groups - 3])
+        pool_group(groups - 4)
+        quantise(len(UNITS) - 3)
+        regroup(last - 1, "scalar")
+        flip_half(last, 0)
+        regroup_half(last, 0, "vector")
+        invert(BATCH_OF[groups - 2])
+        finish(groups - 4)
+        flip_half(last, 1)
+        regroup_half(last, 1, "scalar")
+        pool_group(groups - 3)
+        quantise(len(UNITS) - 2)
+        quantise_half(len(UNITS) - 1, 0)
+        invert(BATCH_OF[groups - 1])
+        pool_group(groups - 2)
+        quantise_half(len(UNITS) - 1, 1)
+        finish(groups - 3)
+        finish(groups - 2)
+        pool_group(groups - 1)
+        finish(groups - 1)

@@ -24,7 +24,7 @@ ONES = [(i, 1) for i in range(NT - GRP, NT)]
 GROUPS = [(i, GRP) for i in range(0, NT - GRP, GRP)] + ONES
 UNITS = [(i, 2) for i in range(0, NT - GRP, 2)] + ONES
 GROUP_OF = {i: g for g, (first, count) in enumerate(GROUPS) for i in range(first, first + count)}
-BATCHES = [(g, 2) for g in range(0, NT // GRP - 2, 2)] + [(g, 1) for g in range(NT // GRP - 2, len(GROUPS))]
+BATCHES = [(g, 4) for g in range(0, 24, 4)] + [(g, 2) for g in range(24, NT // GRP - 2, 2)] + [(g, 1) for g in range(NT // GRP - 2, len(GROUPS))]
 BATCH_OF = {g: b for b, (first, count) in enumerate(BATCHES) for g in range(first, first + count)}
 UNIT_OF = {i: v for v, (first, count) in enumerate(UNITS) for i in range(first, first + count)}
 SCALE = 1.0 / math.sqrt(DK)
@@ -358,12 +358,13 @@ def tile_multiheadedattention_pa_t_kernel(tc, q, k, image_feat, W3, b3, out):
             regrouper = "vector" if step >= EVEN0 and step % 12 == 6 else "scalar"
             if live(ahead):
                 scores(ahead, 0)
+            if step == -LEAD:
+                words_to_k_on_partitions(x_raw, xg, 0, ps_t, "et", nc.scalar.copy)
             if live(ahead):
                 scores(ahead, 1)
             if step == -LEAD:
-                words_to_k_on_partitions(x_raw, xg, 0, ps_t, "et", nc.scalar.copy)
-            if step == 1 - LEAD:
                 prep_q(0, 2, 6, ps_t, "et", nc.scalar.copy)
+            if step == 1 - LEAD:
                 words_to_k_on_partitions(x_raw, xg, 1, ps_t, "et", nc.scalar.copy)
             if live(step - 1):
                 flip(step - 1)
@@ -404,7 +405,7 @@ def tile_multiheadedattention_pa_t_kernel(tc, q, k, image_feat, W3, b3, out):
             if step >= PV0 and pooled < len(GROUPS) and emptied == pooled:
                 first, count = GROUPS[pooled]
                 inverted = sum(GROUPS[sum(BATCHES[BATCH_OF[pooled]]) - 1])
-                if inverted <= step - 2 and (first >= NT - 4 * GRP or step % 4 == 3 or first + 3 * GRP <= step and step % 8 == 5):
+                if inverted <= step - 2 and (step >= NT - 8 or step % 4 == 3 or first + 5 * GRP <= step and step % 8 == 5):
                     for i in range(first, first + count):
                         pool_features(i)
                     pooled += 1

@@ -355,7 +355,7 @@ def tile_multiheadedattention_pa_t_kernel(tc, q, k, image_feat, W3, b3, out):
         quantised = pooled = emptied = 0
         for step in range(-LEAD, NT - 1):
             ahead = step + LEAD
-            regrouper = "vector" if step >= EVEN0 and step % 12 == 6 else "scalar"
+            regrouper = "vector" if step >= EVEN0 and step % 10 == 6 else "scalar"
             if live(ahead):
                 scores(ahead, 0)
             if step == -LEAD:
@@ -378,13 +378,13 @@ def tile_multiheadedattention_pa_t_kernel(tc, q, k, image_feat, W3, b3, out):
                 emptied += 1
             if not late and live(ahead):
                 row_max(ahead, 0)
+            if not late and live(ahead):
+                row_max(ahead, 1)
+            if 0 <= step - 1 < TAIL and regrouper == "vector":
+                regroup(step - 1, regrouper)
             if quantised < len(UNITS) and sum(UNITS[quantised]) <= step - 1:
                 quantise(quantised)
                 quantised += 1
-            if 0 <= step - 1 < TAIL and regrouper == "vector":
-                regroup(step - 1, regrouper)
-            if not late and live(ahead):
-                row_max(ahead, 1)
             if live(ahead):
                 shift(ahead)
             if live(step):
@@ -442,7 +442,7 @@ def tile_multiheadedattention_pa_t_kernel(tc, q, k, image_feat, W3, b3, out):
         quantise(len(UNITS) - 3)
         regroup(last - 1, "scalar")
         flip_half(last, 0)
-        regroup_half(last, 0, "vector")
+        regroup_half(last, 0, "scalar")
         invert(BATCH_OF[groups - 2])
         finish(groups - 4)
         flip_half(last, 1)

@@ -33,7 +33,7 @@ EC_BUFS = 14
 X0, W0, PV0 = 2, 6, 23
 EVEN0 = 24
 PROJECTIONS = [step for step in range(10, 20) if step % 8 != 1 and step != 13]
-WARM = 9
+WARM = 8
 TAIL = NT - 3
 LEAD = 2
 
@@ -352,14 +352,13 @@ def tile_multiheadedattention_pa_t_kernel(tc, q, k, image_feat, W3, b3, out):
         prep_k(0, 0, ps_t, "et", nc.vector.tensor_copy)
         prep_q(0, 0, 2, ps_s, "s", nc.scalar.copy)
         prep_k(0, 1, ps_t, "et", nc.vector.tensor_copy)
+        words_to_k_on_partitions(x_raw, xg, 0, ps_s, "s", nc.scalar.copy)
         quantised = pooled = emptied = 0
         for step in range(-LEAD, NT - 1):
             ahead = step + LEAD
-            regrouper = "vector" if step >= EVEN0 and step % 10 == 6 else "scalar"
+            regrouper = "vector" if step >= EVEN0 and step % 12 == 6 else "scalar"
             if live(ahead):
                 scores(ahead, 0)
-            if step == -LEAD:
-                words_to_k_on_partitions(x_raw, xg, 0, ps_t, "et", nc.scalar.copy)
             if live(ahead):
                 scores(ahead, 1)
             if step == -LEAD:

from contextlib import ExitStack
import math

import concourse.mybir as mybir
from concourse.masks import make_identity

F32 = mybir.dt.float32
BF16 = mybir.dt.bfloat16
U32 = mybir.dt.uint32
U8 = mybir.dt.uint8
FP8X4 = mybir.dt.float8_e4m3fn_x4
ALU = mybir.AluOpType
ACTF = mybir.ActivationFunctionType
AX = mybir.AxisListType

P = 128
H, SQ, SK, DK = 4, 4096, 1024, 128
D = H * DK
NQ = SQ // P
NT = H * NQ
NB = SK // P
GRP = 4
ONES = [(i, 1) for i in range(NT - GRP, NT)]
GROUPS = [(i, GRP) for i in range(0, NT - GRP, GRP)] + ONES
UNITS = [(i, 2) for i in range(0, NT - GRP, 2)] + ONES
GROUP_OF = {i: g for g, (first, count) in enumerate(GROUPS) for i in range(first, first + count)}
BATCHES = [(g, 4) for g in range(0, 24, 4)] + [(g, 2) for g in range(24, NT // GRP - 2, 2)] + [(g, 1) for g in range(NT // GRP - 2, len(GROUPS))]
BATCH_OF = {g: b for b, (first, count) in enumerate(BATCHES) for g in range(first, first + count)}
UNIT_OF = {i: v for v, (first, count) in enumerate(UNITS) for i in range(first, first + count)}
SCALE = 1.0 / math.sqrt(DK)
FLOPS = 2 * SK * D * D + 2 * 2 * H * SQ * SK * DK
EC_BUFS = 14
X0, W0, PV0 = 2, 6, 23
EVEN0 = 24
PROJECTIONS = [step for step in range(10, 20) if step % 8 != 1 and step != 13]
WARM = 8
TAIL = NT - 3
LEAD = 2


def tile_multiheadedattention_pa_t_kernel(tc, q, k, image_feat, W3, b3, out):
    nc = tc.nc
    qf = q.flatten_outer_dims()
    kf = k.flatten_outer_dims()
    xf = image_feat.flatten_outer_dims()
    of = out.flatten_outer_dims()

    with ExitStack() as ctx:
        const = ctx.enter_context(tc.tile_pool(name="const", bufs=1))
        qraw_pool = ctx.enter_context(tc.tile_pool(name="qraw", bufs=H))
        qt_pool = ctx.enter_context(tc.tile_pool(name="qt", bufs=2))
        work = ctx.enter_context(tc.tile_pool(name="work", bufs=5))
        codes = ctx.enter_context(tc.tile_pool(name="codes", bufs=EC_BUFS))
        stat = ctx.enter_context(tc.tile_pool(name="stat", bufs=4))
        sums = ctx.enter_context(tc.tile_pool(name="sums", bufs=8))
        ps_s = ctx.enter_context(tc.psum_pool(name="ps_s", bufs=6))
        ps_t = ctx.enter_context(tc.psum_pool(name="ps_t", bufs=2))

        ident_b = const.tile([P, P], BF16, name="ident_b")
        make_identity(nc, ident_b[:])
        ident_f = const.tile([P, P], F32, name="ident_f")
        make_identity(nc, ident_f[:])

        warm = ps_s.tile([P, P], F32, name="warm", tag="s")
        for n in range(WARM):
            nc.tensor.matmul(out=warm[:], lhsT=ident_b[:], rhs=ident_b[:], start=True, stop=True)

        x_raw = const.tile([P, NB * D], BF16, name="x_raw")
        w_raw = const.tile([P, H * D], BF16, name="w_raw")
        b3bc = const.tile([P, D], BF16, name="b3bc")
        k_raw = const.tile([P, H, NB, DK], BF16, name="k_raw")
        q_raws = []
        for h in range(H):
            k_dst = k_raw[:, h, :, :].rearrange("p (g t) d -> p g (t d)", g=2)
            k_src = kf[h * SK : (h + 1) * SK, :].rearrange("(g p t) d -> p g (t d)", g=2, t=4)
            if h > 0:
                nc.sync.dma_start(out=k_dst, in_=k_src)
            q_raw = qraw_pool.tile([P, NQ, DK], BF16, name="q_raw", tag="q_raw")
            q_src = qf[h * SQ : (h + 1) * SQ, :].rearrange("(p n) d -> p n d", n=NQ)
            if h == 0:
                x_dst = x_raw[:].rearrange("p (g a w) -> p g a w", g=2, a=2)
                x_src = xf.rearrange("(g p a t) c -> p g a (t c)", g=2, a=2, t=2)
                nc.sync.dma_start(out=k_dst[:, 0:1, :], in_=k_src[:, 0:1, :])
                nc.sync.dma_start(out=q_raw[:, 0:2, :], in_=q_src[:, 0:2, :])
                nc.sync.dma_start(out=k_dst[:, 1:2, :], in_=k_src[:, 1:2, :])
                nc.sync.dma_start(out=x_dst[:, 0, 0, :], in_=x_src[:, 0, 0, :])
                nc.sync.dma_start(out=q_raw[:, 2:8, :], in_=q_src[:, 2:8, :])
                nc.sync.dma_start(out=x_dst[:, 0, 1, :], in_=x_src[:, 0, 1, :])
                nc.sync.dma_start(out=x_dst[:, 1, :, :], in_=x_src[:, 1, :, :])
                nc.sync.dma_start(out=q_raw[:, 8:16, :], in_=q_src[:, 8:16, :])
                nc.sync.dma_start(
                    out=w_raw[:].rearrange("p (n c) -> p n c", n=H),
                    in_=W3.rearrange("(n p) c -> p n c", p=P),
                )
                nc.sync.dma_start(out=b3bc[:], in_=b3.partition_broadcast(P))
                nc.sync.dma_start(out=q_raw[:, 16:32, :], in_=q_src[:, 16:32, :])
            else:
                nc.sync.dma_start(out=q_raw[:], in_=q_src)
            q_raws.append(q_raw)

        kT = const.tile([P, H, SK], BF16, name="kT")
        qTs = {}

        def prep_k(h, g, bank, tag, copy):
            pk = bank.tile([P, 4, P], BF16, name="pk", tag=tag)
            for t in range(4):
                nc.tensor.transpose(pk[:, t, :], k_raw[:, h, 4 * g + t, :], ident_b[:])
            copy(
                out=kT[:, h, g * 512 : (g + 1) * 512].rearrange("p (u r e) -> p u r e", u=2, e=2),
                in_=pk[:].rearrange("p (u e) r -> p u r e", e=2),
            )

        def prep_q(h, first, count, bank, tag, copy):
            if first == 0:
                qTs[h] = qt_pool.tile([P, NQ, P], BF16, name="qT", tag="qT")
            pq = bank.tile([P, count, P], BF16, name="pq", tag=tag)
            for a in range(count):
                nc.tensor.transpose(pq[:, a, :], q_raws[h][:, first + a, :], ident_b[:])
            copy(out=qTs[h][:, first : first + count, :], in_=pq[:])

        xg = const.tile([P, SK * 4], BF16, name="xg", align_bytes=64)
        wg = const.tile([P, D * 4], BF16, name="wg", align_bytes=64)
        xc = const.tile([P, SK], U32, name="xc", align_bytes=64)
        xs = const.tile([P, SK], U8, name="xs", align_bytes=64)
        wc = const.tile([P, D], U32, name="wc", align_bytes=64)
        ws = const.tile([P, D], U8, name="ws", align_bytes=64)
        ig = const.tile([P, 2, D, 4], BF16, name="ig", align_bytes=64)
        ic = const.tile([P, 2, D], U32, name="ic", align_bytes=64)
        isc = const.tile([P, 2, D], U8, name="isc", align_bytes=64)

        def words_to_k_on_partitions(raw, grouped, pair, bank, tag, copy):
            raw32 = raw[:].bitcast(F32)
            grouped32 = grouped[:].bitcast(F32)
            px = bank.tile([P, 2, 2, P], F32, name="px", tag=tag)
            for a in range(2):
                for u in range(2):
                    c0 = (2 * pair + a) * (D // 2) + u * P
                    nc.tensor.transpose(px[:, a, u, :], raw32[:, c0 : c0 + P], ident_f[:])
            copy(
                out=grouped32[:, pair * 512 : (pair + 1) * 512].rearrange(
                    "p (a r u) -> p a r u", a=2, u=2
                ),
                in_=px[:].rearrange("p a u r -> p a r u"),
            )

        def quantise_x(half):
            nc.vector.quantize_mx(
                out=xc[:, half * 512 : (half + 1) * 512].bitcast(FP8X4),
                scales=xs[:, half * 512 : (half + 1) * 512],
                in_=xg[:, half * 2048 : (half + 1) * 2048],
            )

        def quantise_w():
            nc.vector.quantize_mx(out=wc[:].bitcast(FP8X4), scales=ws[:], in_=wg[:])

        def project(g, h):
            hs = slice(h * DK, (h + 1) * DK)
            pi = ps_t.tile([P, 4, DK], F32, name="pi", tag="et")
            for t in range(4):
                bs = slice((4 * g + t) * P, (4 * g + t + 1) * P)
                nc.tensor.matmul_mx(
                    out=pi[:, t, :],
                    lhsT=xc[:, bs].bitcast(FP8X4),
                    lhsT_scale=xs[:, bs],
                    rhs=wc[:, hs].bitcast(FP8X4),
                    rhs_scale=ws[:, hs],
                    start=True,
                    stop=True,
                )
            nc.vector.tensor_tensor(
                out=ig[:, g, hs, :],
                in0=pi[:].rearrange("p t o -> p o t"),
                in1=b3bc[:, hs].unsqueeze(2).to_broadcast([P, DK, 4]),
                op=ALU.add,
            )

        def quantise_imf(g):
            nc.vector.quantize_mx(
                out=ic[:, g, :].bitcast(FP8X4),
                scales=isc[:, g, :],
                in_=ig[:, g, :, :].rearrange("p o t -> p (o t)"),
            )

        s_t, nb_t, e_t, et_t, eg_t, ec_t, es_t, rs_t, pv_t = {}, {}, {}, {}, {}, {}, {}, {}, {}
        rsum_t, rcp_t, mx_t = {}, {}, {}

        def scores(i, c):
            h, n = divmod(i, NQ)
            s = ps_s.tile([P, 512], F32, name="s", tag="s")
            nc.tensor.matmul(
                out=s[:],
                lhsT=qTs[h][:, n, :],
                rhs=kT[:, h, c * 512 : (c + 1) * 512],
                start=True,
                stop=True,
            )
            s_t[i, c] = s

        def row_max(i, c):
            if c == 0:
                mx_t[i] = stat.tile([P, 2], F32, name="mx", tag="mx")
            nc.vector.tensor_reduce(out=mx_t[i][:, c : c + 1], in_=s_t[i, c][:], axis=AX.X, op=ALU.max)

        def shift(i):
            mx = mx_t[i]
            nb = stat.tile([P, 1], F32, name="nb", tag="nb")
            nc.gpsimd.tensor_scalar(
                out=nb[:], in0=mx[:, 0:1], scalar1=mx[:, 1:2], scalar2=-SCALE, op0=ALU.max, op1=ALU.mult
            )
            nb_t[i] = nb

        def exponent(i):
            first, count = GROUPS[GROUP_OF[i]]
            if i == first:
                rs_t[GROUP_OF[i]] = sums.tile([P, count, 2], F32, name="rs", tag="rs")
            rs = rs_t[GROUP_OF[i]]
            e = work.tile([P, SK], BF16, name="e", tag="e")
            for c in range(2):
                nc.scalar.activation(
                    out=e[:, c * 512 : (c + 1) * 512],
                    in_=s_t[i, c][:],
                    func=ACTF.Exp,
                    bias=nb_t[i][:],
                    scale=SCALE,
                    accum_out=rs[:, i - first, c : c + 1],
                )
            e_t[i] = e

        def flip(i):
            words = e_t[i][:].bitcast(F32)
            bank, tag = (ps_t, "et") if i < TAIL else (ps_s, "s")
            et = bank.tile([P, 4, P], F32, name="et", tag=tag)
            for m in range(4):
                nc.tensor.transpose(et[:, m, :], words[:, m * P : (m + 1) * P], ident_f[:])
            et_t[i] = et

        def flip_half(i, g):
            words = e_t[i][:].bitcast(F32)
            et = ps_s.tile([P, 2, P], F32, name="et", tag="s")
            for u in range(2):
                m = 2 * g + u
                nc.tensor.transpose(et[:, u, :], words[:, m * P : (m + 1) * P], ident_f[:])
            et_t[i, g] = et

        def regroup(i, engine):
            unit = UNIT_OF[i]
            first, count = UNITS[unit]
            if i == first:
                eg_t[unit] = work.tile([P, count, SK], BF16, name="eg", tag="eg", align_bytes=64)
            copy = nc.vector.tensor_copy if engine == "vector" else nc.scalar.copy
            copy(
                out=eg_t[unit][:, i - first, :].bitcast(F32).rearrange("p (g r u) -> p g r u", g=2, u=2),
                in_=et_t[i][:].rearrange("p (g u) r -> p g r u", g=2),
            )

        def regroup_half(i, g, engine):
            unit = UNIT_OF[i]
            if g == 0:
                eg_t[unit] = work.tile([P, 1, SK], BF16, name="eg", tag="eg", align_bytes=64)
            copy = nc.vector.tensor_copy if engine == "vector" else nc.scalar.copy
            copy(
                out=eg_t[unit][:, 0, g * 512 : (g + 1) * 512].bitcast(F32).rearrange("p (r u) -> p r u", u=2),
                in_=et_t[i, g][:].rearrange("p u r -> p r u"),
            )

        def quantise_half(unit, g):
            if g == 0:
                ec_t[unit] = codes.tile([P, 2 * P], U32, name="ec", tag="ec", align_bytes=64)
                es_t[unit] = codes.tile([P, 2 * P], U8, name="es", tag="es", align_bytes=64)
            bs = slice(g * P, (g + 1) * P)
            nc.vector.quantize_mx(
                out=ec_t[unit][:, bs].bitcast(FP8X4),
                scales=es_t[unit][:, bs],
                in_=eg_t[unit][:, 0, g * 512 : (g + 1) * 512],
            )

        def quantise(unit):
            words = UNITS[unit][1] * 2 * P
            ec = codes.tile([P, words], U32, name="ec", tag="ec", align_bytes=64)
            es = codes.tile([P, words], U8, name="es", tag="es", align_bytes=64)
            nc.vector.quantize_mx(
                out=ec[:].bitcast(FP8X4), scales=es[:], in_=eg_t[unit][:].rearrange("p a k -> p (a k)")
            )
            ec_t[unit] = ec
            es_t[unit] = es

        def pool_features(i):
            h = i // NQ
            grp = GROUP_OF[i]
            first, count = GROUPS[grp]
            if i == first and count == GRP:
                pv_t[grp] = ps_t.tile([P, GRP, DK], F32, name="pv", tag="et")
            elif i == first:
                pv_t[grp] = ps_s.tile([P, count, DK], F32, name="pv", tag="s")
            pv = pv_t[grp]
            hs = slice(h * DK, (h + 1) * DK)
            unit = UNIT_OF[i]
            for g in range(2):
                block = 2 * (i - UNITS[unit][0]) + g
                bs = slice(block * P, (block + 1) * P)
                nc.tensor.matmul_mx(
                    out=pv[:, i - first, :],
                    lhsT=ec_t[unit][:, bs].bitcast(FP8X4),
                    lhsT_scale=es_t[unit][:, bs],
                    rhs=ic[:, g, hs].bitcast(FP8X4),
                    rhs_scale=isc[:, g, hs],
                    start=(g == 0),
                    stop=(g == 1),
                )

        def row_sum(grp):
            count = GROUPS[grp][1]
            batch = BATCH_OF[grp]
            first, groups = BATCHES[batch]
            if grp == first:
                rsum_t[batch] = sums.tile([P, groups, count], F32, name="rsum", tag="rsum")
            nc.gpsimd.tensor_tensor(
                out=rsum_t[batch][:, grp - first, :], in0=rs_t[grp][:, :, 0], in1=rs_t[grp][:, :, 1], op=ALU.add
            )

        def invert(batch):
            first, groups = BATCHES[batch]
            rcp = sums.tile([P, groups, GROUPS[first][1]], F32, name="rcp", tag="rcp")
            nc.vector.reciprocal(out=rcp[:], in_=rsum_t[batch][:])
            rcp_t[batch] = rcp

        def finish(grp):
            first, count = GROUPS[grp]
            h, n = divmod(first, NQ)
            o_sb = work.tile([P, count, DK], F32, name="o_sb", tag="o_sb")
            nc.vector.tensor_tensor(
                out=o_sb[:],
                in0=pv_t[grp][:],
                in1=rcp_t[BATCH_OF[grp]][:, grp - BATCHES[BATCH_OF[grp]][0], :].unsqueeze(2).to_broadcast([P, count, DK]),
                op=ALU.mult,
            )
            nc.sync.dma_start(
                out=of[h * SQ : (h + 1) * SQ, :].rearrange("(p n) d -> p n d", n=NQ)[:, n : n + count, :],
                in_=o_sb[:],
            )

        def live(i):
            return 0 <= i < NT

        def last_of_group(i):
            return i == NT - 1 or GROUP_OF[i + 1] != GROUP_OF[i]

        def last_of_batch(i):
            return last_of_group(i) and sum(BATCHES[BATCH_OF[GROUP_OF[i]]]) == GROUP_OF[i] + 1

        ctx.enter_context(tc.manual_schedule())
        prep_k(0, 0, ps_t, "et", nc.vector.tensor_copy)
        prep_q(0, 0, 2, ps_s, "s", nc.scalar.copy)
        prep_k(0, 1, ps_t, "et", nc.vector.tensor_copy)
        words_to_k_on_partitions(x_raw, xg, 0, ps_s, "s", nc.scalar.copy)
        quantised = pooled = emptied = 0
        for step in range(-LEAD, NT - 1):
            ahead = step + LEAD
            regrouper = "vector" if step >= EVEN0 and step % 12 == 6 else "scalar"
            if live(ahead):
                scores(ahead, 0)
            if live(ahead):
                scores(ahead, 1)
            if step == -LEAD:
                prep_q(0, 2, 6, ps_t, "et", nc.scalar.copy)
            if step == 1 - LEAD:
                words_to_k_on_partitions(x_raw, xg, 1, ps_t, "et", nc.scalar.copy)
            if live(step - 1):
                flip(step - 1)
            late = ahead >= NT - 1
            if late and live(ahead):
                row_max(ahead, 0)
            if late and live(ahead):
                row_max(ahead, 1)
            if emptied < pooled:
                finish(emptied)
                emptied += 1
            if not late and live(ahead):
                row_max(ahead, 0)
            if not late and live(ahead):
                row_max(ahead, 1)
            if 0 <= step - 1 < TAIL and regrouper == "vector":
                regroup(step - 1, regrouper)
            if quantised < len(UNITS) and sum(UNITS[quantised]) <= step - 1:
                quantise(quantised)
                quantised += 1
            if live(ahead):
                shift(ahead)
            if live(step):
                exponent(step)
            if 0 <= step - 1 < TAIL and regrouper == "scalar":
                regroup(step - 1, regrouper)
            if live(step - 1) and last_of_group(step - 1):
                row_sum(GROUP_OF[step - 1])
            if live(step - 2) and last_of_batch(step - 2):
                invert(BATCH_OF[GROUP_OF[step - 2]])
            h, n = divmod(step + 7, NQ)
            if 0 < step + 7 < NT and n % 8 == 0:
                prep_q(h, n, 8, ps_t, "et", nc.vector.tensor_copy)
            for g in range(2):
                h, n = divmod(step + 19 - 8 * g, NQ)
                if 0 < h < H and n == 0:
                    prep_k(h, g, ps_t, "et", nc.scalar.copy)
            if step >= PV0 and pooled < len(GROUPS) and emptied == pooled:
                first, count = GROUPS[pooled]
                inverted = sum(GROUPS[sum(BATCHES[BATCH_OF[pooled]]) - 1])
                if inverted <= step - 2 and (step >= NT - 8 or step % 4 == 3 or first + 5 * GRP <= step and step % 8 == 5):
                    for i in range(first, first + count):
                        pool_features(i)
                    pooled += 1
            if step in (X0 + 1, X0 + 3):
                words_to_k_on_partitions(x_raw, xg, 2 + (step - X0) // 2, ps_t, "et", nc.vector.tensor_copy)
            if step in (X0 + 2, X0 + 4):
                quantise_x((step - X0) // 2 - 1)
            if W0 <= step < W0 + 2:
                words_to_k_on_partitions(w_raw, wg, step - W0, ps_t, "et", nc.scalar.copy)
            if step == W0 + 2:
                quantise_w()
            if step in PROJECTIONS:
                piece = PROJECTIONS.index(step)
                project(piece // 4, piece % 4)
            for g in range(2):
                if step == PROJECTIONS[4 * g + 3] + 1:
                    quantise_imf(g)

        def pool_group(grp):
            first, count = GROUPS[grp]
            for i in range(first, first + count):
                pool_features(i)

        last = NT - 1
        groups = len(GROUPS)
        exponent(last)
        flip(last - 1)
        finish(groups - 5)
        regroup(last - 2, "vector")
        row_sum(groups - 2)
        row_sum(groups - 1)
        invert(BATCH_OF[groups - 3])
        pool_group(groups - 4)
        quantise(len(UNITS) - 3)
        regroup(last - 1, "scalar")
        flip_half(last, 0)
        regroup_half(last, 0, "scalar")
        invert(BATCH_OF[groups - 2])
        finish(groups - 4)
        flip_half(last, 1)
        regroup_half(last, 1, "scalar")
        pool_group(groups - 3)
        quantise(len(UNITS) - 2)
        quantise_half(len(UNITS) - 1, 0)
        invert(BATCH_OF[groups - 1])
        pool_group(groups - 2)
        quantise_half(len(UNITS) - 1, 1)
        finish(groups - 3)
        finish(groups - 2)
        pool_group(groups - 1)
        finish(groups - 1)
